import numpy as np
import ml_dtypes


def mxq(x, axis, fmt="e4m3"):
    dtype, down = {"e4m3": (ml_dtypes.float8_e4m3fn, 7), "e5m2": (ml_dtypes.float8_e5m2, 14)}[fmt]
    v = np.moveaxis(np.asarray(x, np.float32).astype(ml_dtypes.bfloat16).astype(np.float64), axis, -1)
    blocks = v.reshape(v.shape[:-1] + (-1, 32))
    amax = np.abs(blocks).max(-1, keepdims=True)
    byte = np.maximum(np.where(amax > 0, np.frexp(amax)[1] - 1 + 127, 0) - down, 1)
    scale = np.exp2(byte - 127.0)
    codes = (blocks / scale).astype(np.float32).astype(dtype).astype(np.float64)
    return np.moveaxis((codes * scale).reshape(v.shape), -1, axis)


WIDE = False


def mx_kscale(k):
    if not WIDE:
        return np.ones(k)
    levels = np.array([10, -10, 5, -5, 0])
    if k % 512:
        return np.exp2(np.random.permutation(np.resize(levels, k // 32))).repeat(32)
    a = np.empty((k // 512, 16))
    for p in range(k // 512):
        a[p, :8] = np.random.permutation(np.resize(levels, 8))
        for g in range(8):
            far = levels[np.abs(levels - a[p, g]) >= 10]
            a[p, g + 8] = far[np.random.randint(len(far))]
    return np.exp2(a.ravel()).repeat(32)


BF16 = ml_dtypes.bfloat16


def bf(x):
    return np.asarray(x, np.float32).astype(BF16)


def f64(x):
    return np.asarray(x).astype(np.float64)


N, DIN, H1, H2, C, NC, G = 1024, 512, 512, 256, 128, 512, 8


def draw0():
    s, t = mx_kscale(N), mx_kscale(DIN)
    return {"F_": bf(np.random.uniform(size=(N, N)) * 2.0 / np.sqrt(N) * s),
            "X": bf(np.random.standard_normal((N, DIN)) / s[:, None] * t),
            "W1": bf(np.random.standard_normal((DIN, H1)) * 0.8 / np.sqrt(DIN) / t[:, None]),
            "b1": bf(np.random.standard_normal(H1) * 0.3)}


def core(F_, X, W1, b1):
    agg = mxq(f64(F_), 1, "e4m3") @ mxq(f64(X), 0, "e4m3")
    return np.tanh((mxq(agg, 1, "e4m3") @ mxq(f64(W1), 0, "e4m3")) + f64(b1))


def e4m3fn_bytes(y):
    return np.clip(np.asarray(y, np.float64), -448.0, 448.0).astype(np.float32).astype(ml_dtypes.float8_e4m3fn).view(np.uint8)


def e4m3fn_values(b):
    return np.asarray(b, np.uint8).view(ml_dtypes.float8_e4m3fn).astype(np.float64)


def setup_inputs():
    d = draw0()
    x0 = np.asarray(d['F_']).astype(np.float64)
    s = (np.max(np.abs(x0), axis=(0,), keepdims=True) / 448.0).astype(np.float32)
    out = {}
    for k, v in d.items():
        if k == 'F_':
            out['F__bytes'] = e4m3fn_bytes(x0 / s.astype(np.float64))
            out['F__scale'] = s
        else:
            out[k] = v
    return out


def reference(F__bytes, F__scale, X, W1, b1):
    return core(e4m3fn_values(F__bytes) * F__scale.astype(np.float64), X, W1, b1)

@@ -1,0 +1,283 @@
+from contextlib import ExitStack
+
+import concourse.mybir as mybir
+from concourse.masks import make_identity
+
+NODES, FEATS, HID = 1024, 512, 512
+FLOPS = 2 * NODES * NODES * FEATS + 2 * NODES * FEATS * HID
+
+F32 = mybir.dt.float32
+BF16 = mybir.dt.bfloat16
+U32 = mybir.dt.uint32
+U8 = mybir.dt.uint8
+FP8 = mybir.dt.float8_e4m3fn
+FP8X4 = mybir.dt.float8_e4m3fn_x4
+ACT = mybir.ActivationFunctionType
+ALU = mybir.AluOpType
+
+P = 128
+NB = 8
+NG = 2
+VIA_GPSIMD = ()
+
+
+def tile_controencodnet_pa_kernel(tc, f_bytes, f_scale, x, w1, b1, out):
+    nc = tc.nc
+    f_view = f_bytes.rearrange("(p b) k -> p b k", b=NB)
+    o_view = out.rearrange("(p b) h -> p b h", b=NB)
+
+    with ExitStack() as ctx:
+        keep = ctx.enter_context(tc.tile_pool(name="keep", bufs=1))
+        work = ctx.enter_context(tc.tile_pool(name="work", bufs=3))
+        pst = ctx.enter_context(tc.psum_pool(name="pst", bufs=2))
+        psa = ctx.enter_context(tc.psum_pool(name="psa", bufs=2))
+        pso = ctx.enter_context(tc.psum_pool(name="pso", bufs=4))
+        ctx.enter_context(tc.manual_schedule())
+
+        raw = [keep.tile([P, 1, NODES], U8, name="raw0"), keep.tile([P, 1, NODES], U8, name="raw1")]
+        raw += [keep.tile([P, 2, NODES], U8, name="raw%d" % i) for i in (2, 4, 6)]
+
+        def bytes_of(b):
+            if b < 2:
+                return raw[b][:, 0, :]
+            return raw[1 + b // 2][:, b % 2, :]
+
+        scale = keep.tile([P, NG, 2, 2], F32)
+        nc.scalar.dma_start(
+            out=scale[:].rearrange("p g u e -> p g (u e)"),
+            in_=f_scale.rearrange("o (g p t) -> p (o g) t", p=P, t=4),
+        )
+        dummy = keep.tile([P, 1], F32)
+        dummy2 = keep.tile([P, 1], F32)
+        nc.vector.memset(dummy[:], 0.0)
+        nc.scalar.activation(out=dummy2[:], in_=dummy[:], func=ACT.Tanh)
+
+        nc.sync.dma_start(out=raw[0][:], in_=f_view[:, 0:1, :])
+        nc.sync.dma_start(out=raw[1][:], in_=f_view[:, 1:2, :])
+        nc.sync.dma_start(out=raw[2][:], in_=f_view[:, 2:4, :])
+        x_raw = [keep.tile([P, 4, FEATS], BF16, name="x_raw%d" % g) for g in range(NG)]
+        x_view = x.rearrange("(g p j) n -> g p j n", p=P, j=4)
+        for g in range(NG):
+            nc.sync.dma_start(out=x_raw[g][:], in_=x_view[g])
+        nc.sync.dma_start(out=raw[3][:], in_=f_view[:, 4:6, :])
+        nc.sync.dma_start(out=raw[4][:], in_=f_view[:, 6:8, :])
+        w_raw = keep.tile([P, 4, HID], BF16)
+        nc.sync.dma_start(out=w_raw[:], in_=w1.rearrange("(p j) n -> p j n", j=4))
+        bias = keep.tile([P, HID], BF16)
+        nc.sync.dma_start(out=bias[:], in_=b1.partition_broadcast(P))
+
+        ident = keep.tile([P, P], F32)
+        make_identity(nc, ident[:])
+
+        x_codes = [keep.tile([P, FEATS], U32, name="x_codes%d" % g, align_bytes=64) for g in range(NG)]
+        x_scales = [keep.tile([P, FEATS], U8, name="x_scales%d" % g, align_bytes=64) for g in range(NG)]
+        x_grp = [keep.tile([P, 4, P, 4], BF16, name="x_grp%d" % g, align_bytes=64) for g in range(NG)]
+        w_codes = keep.tile([P, HID], U32, align_bytes=64)
+        w_scales = keep.tile([P, HID], U8, align_bytes=64)
+        w_grp = keep.tile([P, 4 * HID], BF16, align_bytes=64)
+
+        st = {}
+
+        def cast(b):
+            t = work.tile([P, NODES], BF16, name="f_bf", align_bytes=64, bufs=8)
+            if b < 2:
+                nc.vector.tensor_copy(out=t[:], in_=bytes_of(b).bitcast(FP8))
+            else:
+                nc.scalar.copy(out=t[:], in_=bytes_of(b).bitcast(FP8))
+            st["c", b] = t
+
+        def turn(b):
+            t = pst.tile([P, 2, NG, P], F32, name="f_t")
+            words = st["c", b][:].bitcast(F32)
+            for g in range(NG):
+                for u in range(2):
+                    nc.tensor.transpose(t[:, u, g, :], words[:, 256 * g + u : 256 * (g + 1) : 2], ident[:])
+            st["t", b] = t
+
+        def mul(b):
+            t = work.tile([P, NG, P, 2, 2], BF16, name="f_grp", align_bytes=64, bufs=4)
+            scales = scale[:].unsqueeze(2).to_broadcast([P, NG, P, 2, 2])
+            if b in VIA_GPSIMD:
+                w = work.tile([P, NG, P, 2], F32, name="f_words", align_bytes=64)
+                nc.scalar.copy(out=w[:], in_=st["t", b][:].rearrange("p u g r -> p g r u"))
+                nc.gpsimd.tensor_tensor(
+                    out=t[:],
+                    in0=w[:].rearrange("p g r u -> p (g r u)").bitcast(BF16).rearrange("p (g r u e) -> p g r u e", g=NG, r=P, u=2),
+                    in1=scales,
+                    op=ALU.mult,
+                )
+            else:
+                nc.vector.tensor_tensor(
+                    out=t[:],
+                    in0=st["t", b][:].rearrange("p u g r -> p (u g r)").bitcast(BF16).rearrange("p (u g r e) -> p g r u e", u=2, g=NG, e=2),
+                    in1=scales,
+                    op=ALU.mult,
+                )
+            st["g", b] = t
+
+        def quant_f(b):
+            q = work.tile([P, NG * P], U32, name="f_codes", align_bytes=64, bufs=8)
+            s = work.tile([P, NG * P], U8, name="f_scales", align_bytes=64, bufs=8)
+            nc.vector.quantize_mx(out=q[:].bitcast(FP8X4), scales=s[:], in_=st["g", b][:].rearrange("p g r u e -> p (g r u e)"))
+            st["q", b] = (q, s)
+
+        def mm1(b):
+            q, s = st["q", b]
+            acc = psa.tile([P, 4, P], F32, name="agg_ps")
+            for t in range(4):
+                for g in range(NG):
+                    nc.tensor.matmul_mx(
+                        out=acc[:, t, :],
+                        lhsT=x_codes[g][:, t * P : (t + 1) * P].bitcast(FP8X4),
+                        lhsT_scale=x_scales[g][:, t * P : (t + 1) * P],
+                        rhs=q[:, g * P : (g + 1) * P].bitcast(FP8X4),
+                        rhs_scale=s[:, g * P : (g + 1) * P],
+                        start=(g == 0),
+                        stop=(g == NG - 1),
+                    )
+            st["a", b] = acc
+
+        def copy_agg(b):
+            t = work.tile([P, P, 4], BF16, name="a_grp", align_bytes=64, bufs=4)
+            nc.scalar.copy(out=t[:], in_=st["a", b][:].rearrange("p t m -> p m t"))
+            st["ag", b] = t
+
+        def quant_a(b):
+            q = work.tile([P, P], U32, name="a_codes", align_bytes=64, bufs=4)
+            s = work.tile([P, P], U8, name="a_scales", align_bytes=64, bufs=4)
+            nc.vector.quantize_mx(out=q[:].bitcast(FP8X4), scales=s[:], in_=st["ag", b][:].rearrange("p m t -> p (m t)"))
+            st["aq", b] = (q, s)
+
+        def mm2(b):
+            q, s = st["aq", b]
+            acc = pso.tile([P, HID], F32, name="out_ps")
+            nc.tensor.matmul_mx(
+                out=acc[:], lhsT=q[:].bitcast(FP8X4), lhsT_scale=s[:], rhs=w_codes[:].bitcast(FP8X4), rhs_scale=w_scales[:], start=True, stop=True
+            )
+            st["o", b] = acc
+
+        def add_bias(b, lo=0, hi=HID):
+            if ("p", b) not in st:
+                st["p", b] = work.tile([P, HID], F32, name="pre", bufs=8)
+            nc.vector.tensor_tensor(out=st["p", b][:, lo:hi], in0=st["o", b][:, lo:hi], in1=bias[:, lo:hi], op=ALU.add)
+
+        def finish(b, lo=0, hi=HID):
+            t = work.tile([P, HID], F32, name="res", bufs=4)
+            nc.scalar.activation(out=t[:, lo:hi], in_=st["p", b][:, lo:hi], func=ACT.Tanh)
+            nc.sync.dma_start(out=o_view[:, b, lo:hi], in_=t[:, lo:hi])
+
+        def group_x(g, m0, m1, engine):
+            dst = x_grp[g][:, :, m0:m1]
+            src = x_raw[g][:].rearrange("p j (m t) -> p t m j", t=4)[:, :, m0:m1]
+            if engine == "S":
+                nc.scalar.copy(out=dst, in_=src)
+            elif engine == "V":
+                nc.vector.tensor_copy(out=dst, in_=src)
+            else:
+                nc.gpsimd.tensor_scalar(out=dst, in0=src, scalar1=1.0, scalar2=0.0, op0=ALU.mult, op1=ALU.add)
+
+        def quant_x(g):
+            nc.vector.quantize_mx(out=x_codes[g][:].bitcast(FP8X4), scales=x_scales[g][:], in_=x_grp[g][:].rearrange("p t m j -> p (t m j)"))
+
+        def group_w(n0, n1, engine):
+            dst = w_grp[:].rearrange("p (n j) -> p n j", j=4)[:, n0:n1]
+            src = w_raw[:].rearrange("p j n -> p n j")[:, n0:n1]
+            if engine == "S":
+                nc.scalar.copy(out=dst, in_=src)
+            else:
+                nc.gpsimd.tensor_scalar(out=dst, in0=src, scalar1=1.0, scalar2=0.0, op0=ALU.mult, op1=ALU.add)
+
+        def quant_w():
+            nc.vector.quantize_mx(out=w_codes[:].bitcast(FP8X4), scales=w_scales[:], in_=w_grp[:])
+
+        cast(0)
+        cast(1)
+        turn(0)
+        cast(2)
+        turn(1)
+        mul(0)
+        group_x(0, 0, 48, "G")
+        group_x(0, 48, 128, "S")
+        mul(1)
+        turn(2)
+        group_x(1, 0, 48, "G")
+        cast(3)
+        quant_x(0)
+        cast(4)
+        mul(2)
+        turn(3)
+        group_w(0, 192, "G")
+        group_x(1, 48, 128, "S")
+        turn(4)
+        mul(3)
+        quant_f(0)
+        cast(5)
+        quant_x(1)
+        mul(4)
+        group_w(192, 512, "S")
+        turn(5)
+        quant_f(1)
+        quant_f(2)
+        mm1(0)
+        quant_f(3)
+        cast(6)
+        mul(5)
+        mm1(1)
+        copy_agg(0)
+        quant_w()
+        quant_a(0)
+        quant_f(4)
+        quant_f(5)
+        turn(6)
+        copy_agg(1)
+        mm1(2)
+        cast(7)
+        mul(6)
+        mm2(0)
+        mm1(3)
+        copy_agg(2)
+        quant_a(1)
+        add_bias(0)
+        turn(7)
+        copy_agg(3)
+        quant_a(2)
+        quant_f(6)
+        mm1(4)
+        finish(0)
+        mul(7)
+        mm2(1)
+        copy_agg(4)
+        mm1(5)
+        add_bias(1)
+        mm2(2)
+        copy_agg(5)
+        quant_f(7)
+        mm1(6)
+        quant_a(3)
+        add_bias(2)
+        finish(1)
+        mm2(3)
+        quant_a(4)
+        mm1(7)
+        copy_agg(6)
+        add_bias(3)
+        finish(2)
+        mm2(4)
+        quant_a(5)
+        add_bias(4)
+        mm2(5)
+        copy_agg(7)
+        quant_a(6)
+        finish(3)
+        add_bias(5)
+        mm2(6)
+        finish(4)
+        quant_a(7)
+        add_bias(6)
+        mm2(7)
+        finish(5)
+        add_bias(7, 0, HID // 2)
+        add_bias(7, HID // 2, HID)
+        finish(6)
+        finish(7, 0, HID // 2)
+        finish(7, HID // 2, HID)

@@ -18,116 +18,133 @@ ALU = mybir.AluOpType
 P = 128
 NB = 8
 NG = 2
-VIA_GPSIMD = ()
 
 
 def tile_controencodnet_pa_kernel(tc, f_bytes, f_scale, x, w1, b1, out):
     nc = tc.nc
     f_view = f_bytes.rearrange("(p b) k -> p b k", b=NB)
     o_view = out.rearrange("(p b) h -> p b h", b=NB)
+    x_view = x.rearrange("(g p j) n -> g p j n", p=P, j=4)
 
     with ExitStack() as ctx:
         keep = ctx.enter_context(tc.tile_pool(name="keep", bufs=1))
-        work = ctx.enter_context(tc.tile_pool(name="work", bufs=3))
-        pst = ctx.enter_context(tc.psum_pool(name="pst", bufs=2))
-        psa = ctx.enter_context(tc.psum_pool(name="psa", bufs=2))
-        pso = ctx.enter_context(tc.psum_pool(name="pso", bufs=4))
+        work = ctx.enter_context(tc.tile_pool(name="work", bufs=NB))
+        psum = ctx.enter_context(tc.psum_pool(name="psum", bufs=1))
         ctx.enter_context(tc.manual_schedule())
 
-        raw = [keep.tile([P, 1, NODES], U8, name="raw0"), keep.tile([P, 1, NODES], U8, name="raw1")]
-        raw += [keep.tile([P, 2, NODES], U8, name="raw%d" % i) for i in (2, 4, 6)]
+        st = {}
 
-        def bytes_of(b):
-            if b < 2:
-                return raw[b][:, 0, :]
-            return raw[1 + b // 2][:, b % 2, :]
+        def bank(kind, dtype=F32, cols=512):
+            return psum.tile([P, cols], dtype, name="bank", bufs=8)
 
-        scale = keep.tile([P, NG, 2, 2], F32)
+        def move(e, dst, src):
+            if e == "S":
+                nc.scalar.copy(out=dst, in_=src)
+            elif e == "V":
+                nc.vector.tensor_copy(out=dst, in_=src)
+            else:
+                nc.gpsimd.tensor_scalar(out=dst, in0=src, scalar1=1.0, scalar2=0.0, op0=ALU.mult, op1=ALU.add)
+
+        scale = keep.tile([P, NG, 2, 2], F32, name="scale")
         nc.scalar.dma_start(
             out=scale[:].rearrange("p g u e -> p g (u e)"),
             in_=f_scale.rearrange("o (g p t) -> p (o g) t", p=P, t=4),
         )
-        dummy = keep.tile([P, 1], F32)
-        dummy2 = keep.tile([P, 1], F32)
+        dummy = keep.tile([P, 1], F32, name="dummy")
+        dummy2 = keep.tile([P, 1], F32, name="dummy2")
         nc.vector.memset(dummy[:], 0.0)
         nc.scalar.activation(out=dummy2[:], in_=dummy[:], func=ACT.Tanh)
 
-        nc.sync.dma_start(out=raw[0][:], in_=f_view[:, 0:1, :])
-        nc.sync.dma_start(out=raw[1][:], in_=f_view[:, 1:2, :])
-        nc.sync.dma_start(out=raw[2][:], in_=f_view[:, 2:4, :])
-        x_raw = [keep.tile([P, 4, FEATS], BF16, name="x_raw%d" % g) for g in range(NG)]
-        x_view = x.rearrange("(g p j) n -> g p j n", p=P, j=4)
-        for g in range(NG):
-            nc.sync.dma_start(out=x_raw[g][:], in_=x_view[g])
-        nc.sync.dma_start(out=raw[3][:], in_=f_view[:, 4:6, :])
-        nc.sync.dma_start(out=raw[4][:], in_=f_view[:, 6:8, :])
-        w_raw = keep.tile([P, 4, HID], BF16)
-        nc.sync.dma_start(out=w_raw[:], in_=w1.rearrange("(p j) n -> p j n", j=4))
-        bias = keep.tile([P, HID], BF16)
-        nc.sync.dma_start(out=bias[:], in_=b1.partition_broadcast(P))
+        def load_f(b0, b1_):
+            t = keep.tile([P, b1_ - b0, NODES], U8, name="raw%d" % b0)
+            nc.sync.dma_start(out=t[:], in_=f_view[:, b0:b1_, :])
+            for b in range(b0, b1_):
+                st["r", b] = t[:, b - b0, :]
 
-        ident = keep.tile([P, P], F32)
+        x_raw = [keep.tile([P, 4, FEATS], BF16, name="x_raw%d" % g) for g in range(NG)]
+        w_raw = keep.tile([P, 4, HID], BF16, name="w_raw")
+        bias = keep.tile([P, HID], BF16, name="bias")
+
+        def load_x(g):
+            nc.sync.dma_start(out=x_raw[g][:], in_=x_view[g])
+
+        def load_w():
+            rows = w1.rearrange("(a t i) n -> t a i n", t=4, i=8)
+            for t in range(4):
+                nc.sync.dma_start(out=w_raw[:, t, :], in_=rows[t])
+
+        def load_b():
+            nc.sync.dma_start(out=bias[:], in_=b1.partition_broadcast(P))
+
+        ident = keep.tile([P, P], F32, name="ident")
         make_identity(nc, ident[:])
 
         x_codes = [keep.tile([P, FEATS], U32, name="x_codes%d" % g, align_bytes=64) for g in range(NG)]
         x_scales = [keep.tile([P, FEATS], U8, name="x_scales%d" % g, align_bytes=64) for g in range(NG)]
-        x_grp = [keep.tile([P, 4, P, 4], BF16, name="x_grp%d" % g, align_bytes=64) for g in range(NG)]
-        w_codes = keep.tile([P, HID], U32, align_bytes=64)
-        w_scales = keep.tile([P, HID], U8, align_bytes=64)
-        w_grp = keep.tile([P, 4 * HID], BF16, align_bytes=64)
+        x_grp = [keep.tile([P, 4, P, 4], BF16, name="grp", align_bytes=64, bufs=2) for g in range(NG)]
+        w_codes = keep.tile([P, HID], U32, name="w_codes", align_bytes=64)
+        w_scales = keep.tile([P, HID], U8, name="w_scales", align_bytes=64)
 
-        st = {}
+        def cast(b, e, lo=0, hi=NODES):
+            if ("c", b) not in st:
+                st["c", b] = work.tile([P, NODES], BF16, name="f_bf", align_bytes=64)
+            move(e, st["c", b][:, lo:hi], st["r", b][:, lo:hi].bitcast(FP8))
 
-        def cast(b):
-            t = work.tile([P, NODES], BF16, name="f_bf", align_bytes=64, bufs=8)
-            if b < 2:
-                nc.vector.tensor_copy(out=t[:], in_=bytes_of(b).bitcast(FP8))
-            else:
-                nc.scalar.copy(out=t[:], in_=bytes_of(b).bitcast(FP8))
-            st["c", b] = t
+        def spread_t(g):
+            t = bank("t")
+            col = scale[:].rearrange("p g u e -> p g (u e)")
+            for j in range(4):
+                nc.tensor.transpose(t[:, j * P : (j + 1) * P], col[:, g, j : j + 1].to_broadcast([P, P]), ident[:])
+            st["sp", g] = t
 
         def turn(b):
-            t = pst.tile([P, 2, NG, P], F32, name="f_t")
-            words = st["c", b][:].bitcast(F32)
+            t = bank("t")
+            words_ = st["c", b][:].bitcast(F32)
             for g in range(NG):
                 for u in range(2):
-                    nc.tensor.transpose(t[:, u, g, :], words[:, 256 * g + u : 256 * (g + 1) : 2], ident[:])
+                    nc.tensor.transpose(t[:, (2 * u + g) * P : (2 * u + g + 1) * P], words_[:, 256 * g + u : 256 * (g + 1) : 2], ident[:])
             st["t", b] = t
 
+        def turn_h(b, g):
+            t = bank("t")
+            words_ = st["c", b][:].bitcast(F32)
+            for u in range(2):
+                nc.tensor.transpose(t[:, u * P : (u + 1) * P], words_[:, 256 * g + u : 256 * (g + 1) : 2], ident[:])
+            st["th", b, g] = t
+
+        def mul_h(b, g):
+            if ("g", b) not in st:
+                st["g", b] = work.tile([P, NG, P, 2, 2], BF16, name="f_grp", align_bytes=64)
+            nc.vector.tensor_tensor(
+                out=st["g", b][:, g],
+                in0=st["th", b, g][:, 0 : 2 * P].bitcast(BF16).rearrange("p (u r e) -> p r u e", u=2, e=2),
+                in1=scale[:, g].unsqueeze(1).to_broadcast([P, P, 2, 2]),
+                op=ALU.mult,
+            )
+
         def mul(b):
-            t = work.tile([P, NG, P, 2, 2], BF16, name="f_grp", align_bytes=64, bufs=4)
-            scales = scale[:].unsqueeze(2).to_broadcast([P, NG, P, 2, 2])
-            if b in VIA_GPSIMD:
-                w = work.tile([P, NG, P, 2], F32, name="f_words", align_bytes=64)
-                nc.scalar.copy(out=w[:], in_=st["t", b][:].rearrange("p u g r -> p g r u"))
-                nc.gpsimd.tensor_tensor(
-                    out=t[:],
-                    in0=w[:].rearrange("p g r u -> p (g r u)").bitcast(BF16).rearrange("p (g r u e) -> p g r u e", g=NG, r=P, u=2),
-                    in1=scales,
-                    op=ALU.mult,
-                )
-            else:
-                nc.vector.tensor_tensor(
-                    out=t[:],
-                    in0=st["t", b][:].rearrange("p u g r -> p (u g r)").bitcast(BF16).rearrange("p (u g r e) -> p g r u e", u=2, g=NG, e=2),
-                    in1=scales,
-                    op=ALU.mult,
-                )
+            t = work.tile([P, NG, P, 2, 2], BF16, name="f_grp", align_bytes=64)
+            nc.vector.tensor_tensor(
+                out=t[:],
+                in0=st["t", b][:].bitcast(BF16).rearrange("p (u g r e) -> p g r u e", u=2, g=NG, e=2),
+                in1=scale[:].unsqueeze(2).to_broadcast([P, NG, P, 2, 2]),
+                op=ALU.mult,
+            )
             st["g", b] = t
 
         def quant_f(b):
-            q = work.tile([P, NG * P], U32, name="f_codes", align_bytes=64, bufs=8)
-            s = work.tile([P, NG * P], U8, name="f_scales", align_bytes=64, bufs=8)
+            q = work.tile([P, NG * P], U32, name="f_codes", align_bytes=64)
+            s = work.tile([P, NG * P], U8, name="f_scales", align_bytes=64)
             nc.vector.quantize_mx(out=q[:].bitcast(FP8X4), scales=s[:], in_=st["g", b][:].rearrange("p g r u e -> p (g r u e)"))
             st["q", b] = (q, s)
 
         def mm1(b):
             q, s = st["q", b]
-            acc = psa.tile([P, 4, P], F32, name="agg_ps")
+            acc = bank("a")
             for t in range(4):
                 for g in range(NG):
                     nc.tensor.matmul_mx(
-                        out=acc[:, t, :],
+                        out=acc[:, t * P : (t + 1) * P],
                         lhsT=x_codes[g][:, t * P : (t + 1) * P].bitcast(FP8X4),
                         lhsT_scale=x_scales[g][:, t * P : (t + 1) * P],
                         rhs=q[:, g * P : (g + 1) * P].bitcast(FP8X4),
@@ -137,20 +154,20 @@ def tile_controencodnet_pa_kernel(tc, f_bytes, f_scale, x, w1, b1, out):
                     )
             st["a", b] = acc
 
-        def copy_agg(b):
-            t = work.tile([P, P, 4], BF16, name="a_grp", align_bytes=64, bufs=4)
-            nc.scalar.copy(out=t[:], in_=st["a", b][:].rearrange("p t m -> p m t"))
+        def copy_agg(b, e="S"):
+            t = work.tile([P, P, 4], BF16, name="a_grp", align_bytes=64)
+            move(e, t[:], st["a", b][:].rearrange("p (t m) -> p m t", t=4))
             st["ag", b] = t
 
         def quant_a(b):
-            q = work.tile([P, P], U32, name="a_codes", align_bytes=64, bufs=4)
-            s = work.tile([P, P], U8, name="a_scales", align_bytes=64, bufs=4)
+            q = work.tile([P, P], U32, name="a_codes", align_bytes=64)
+            s = work.tile([P, P], U8, name="a_scales", align_bytes=64)
             nc.vector.quantize_mx(out=q[:].bitcast(FP8X4), scales=s[:], in_=st["ag", b][:].rearrange("p m t -> p (m t)"))
             st["aq", b] = (q, s)
 
         def mm2(b):
             q, s = st["aq", b]
-            acc = pso.tile([P, HID], F32, name="out_ps")
+            acc = bank("o")
             nc.tensor.matmul_mx(
                 out=acc[:], lhsT=q[:].bitcast(FP8X4), lhsT_scale=s[:], rhs=w_codes[:].bitcast(FP8X4), rhs_scale=w_scales[:], start=True, stop=True
             )
@@ -158,126 +175,130 @@ def tile_controencodnet_pa_kernel(tc, f_bytes, f_scale, x, w1, b1, out):
 
         def add_bias(b, lo=0, hi=HID):
             if ("p", b) not in st:
-                st["p", b] = work.tile([P, HID], F32, name="pre", bufs=8)
+                st["p", b] = work.tile([P, HID], F32, name="pre")
             nc.vector.tensor_tensor(out=st["p", b][:, lo:hi], in0=st["o", b][:, lo:hi], in1=bias[:, lo:hi], op=ALU.add)
 
         def finish(b, lo=0, hi=HID):
-            t = work.tile([P, HID], F32, name="res", bufs=4)
+            if ("y", b) not in st:
+                st["y", b] = work.tile([P, HID], F32, name="res")
+            t = st["y", b]
             nc.scalar.activation(out=t[:, lo:hi], in_=st["p", b][:, lo:hi], func=ACT.Tanh)
             nc.sync.dma_start(out=o_view[:, b, lo:hi], in_=t[:, lo:hi])
 
-        def group_x(g, m0, m1, engine):
-            dst = x_grp[g][:, :, m0:m1]
-            src = x_raw[g][:].rearrange("p j (m t) -> p t m j", t=4)[:, :, m0:m1]
-            if engine == "S":
-                nc.scalar.copy(out=dst, in_=src)
-            elif engine == "V":
-                nc.vector.tensor_copy(out=dst, in_=src)
-            else:
-                nc.gpsimd.tensor_scalar(out=dst, in0=src, scalar1=1.0, scalar2=0.0, op0=ALU.mult, op1=ALU.add)
+        def group_x(g, m0, m1, e):
+            dst = x_grp[g][:].rearrange("p t (a i) j -> p a t i j", i=8)[:, m0 // 8 : m1 // 8]
+            move(e, dst, x_raw[g][:].rearrange("p j (a t i) -> p a t i j", t=4, i=8)[:, m0 // 8 : m1 // 8])
 
         def quant_x(g):
             nc.vector.quantize_mx(out=x_codes[g][:].bitcast(FP8X4), scales=x_scales[g][:], in_=x_grp[g][:].rearrange("p t m j -> p (t m j)"))
 
-        def group_w(n0, n1, engine):
-            dst = w_grp[:].rearrange("p (n j) -> p n j", j=4)[:, n0:n1]
-            src = w_raw[:].rearrange("p j n -> p n j")[:, n0:n1]
-            if engine == "S":
-                nc.scalar.copy(out=dst, in_=src)
-            else:
-                nc.gpsimd.tensor_scalar(out=dst, in0=src, scalar1=1.0, scalar2=0.0, op0=ALU.mult, op1=ALU.add)
+        def group_w(n0, n1, e):
+            if "wg" not in st:
+                st["wg"] = keep.tile([P, 4 * HID], BF16, name="wgrp", align_bytes=64)
+            move(e, st["wg"][:].rearrange("p (n j) -> p n j", j=4)[:, n0:n1], w_raw[:].rearrange("p j n -> p n j")[:, n0:n1])
 
         def quant_w():
-            nc.vector.quantize_mx(out=w_codes[:].bitcast(FP8X4), scales=w_scales[:], in_=w_grp[:])
+            nc.vector.quantize_mx(out=w_codes[:].bitcast(FP8X4), scales=w_scales[:], in_=st["wg"][:])
 
-        cast(0)
-        cast(1)
-        turn(0)
-        cast(2)
-        turn(1)
-        mul(0)
-        group_x(0, 0, 48, "G")
-        group_x(0, 48, 128, "S")
-        mul(1)
-        turn(2)
-        group_x(1, 0, 48, "G")
-        cast(3)
-        quant_x(0)
-        cast(4)
-        mul(2)
-        turn(3)
-        group_w(0, 192, "G")
+        load_f(0, 1)
+        load_f(1, 2)
+        load_f(2, 4)
+        load_x(0)
+        load_x(1)
+        load_f(4, 6)
+        load_f(6, 8)
+        load_w()
+        load_b()
+        cast(0, "V", 0, 512)
+        cast(0, "S", 512, 1024)
+        cast(1, "S")
+        cast(2, "S")
+        cast(3, "S")
+        group_x(0, 64, 128, "S")
+        cast(4, "S")
         group_x(1, 48, 128, "S")
+        cast(5, "S")
+        cast(6, "S")
+        cast(7, "S")
+        group_w(0, 512, "S")
+        turn_h(0,0)
+        turn_h(0,1)
+        turn(1)
+        turn(2)
+        turn(3)
         turn(4)
-        mul(3)
-        quant_f(0)
-        cast(5)
-        quant_x(1)
-        mul(4)
-        group_w(192, 512, "S")
         turn(5)
+        group_x(0, 0, 64, "G")
+        group_x(1, 0, 48, "G")
+        mul_h(0,0)
+        mul_h(0,1)
+        mul(1)
+        mul(2)
+        mul(3)
+        quant_x(0)
+        quant_f(0)
         quant_f(1)
+        quant_x(1)
         quant_f(2)
-        mm1(0)
         quant_f(3)
-        cast(6)
+        mul(4)
         mul(5)
-        mm1(1)
-        copy_agg(0)
-        quant_w()
-        quant_a(0)
         quant_f(4)
-        quant_f(5)
+        quant_w()
+        mm1(0)
         turn(6)
-        copy_agg(1)
-        mm1(2)
-        cast(7)
-        mul(6)
-        mm2(0)
-        mm1(3)
-        copy_agg(2)
-        quant_a(1)
-        add_bias(0)
         turn(7)
+        mm1(1)
+        mm1(2)
+        mm1(3)
+        copy_agg(0)
+        copy_agg(1)
+        copy_agg(2)
         copy_agg(3)
+        quant_a(0)
+        mul(6)
+        quant_f(5)
+        quant_a(1)
         quant_a(2)
-        quant_f(6)
+        mm2(0)
         mm1(4)
-        finish(0)
-        mul(7)
         mm2(1)
-        copy_agg(4)
         mm1(5)
-        add_bias(1)
-        mm2(2)
-        copy_agg(5)
-        quant_f(7)
-        mm1(6)
+        add_bias(0)
+        quant_f(6)
+        mul(7)
         quant_a(3)
-        add_bias(2)
-        finish(1)
+        add_bias(1)
+        quant_f(7)
+        copy_agg(4)
+        finish(0)
+        copy_agg(5)
+        mm1(6)
+        mm2(2)
         mm2(3)
-        quant_a(4)
         mm1(7)
-        copy_agg(6)
-        add_bias(3)
-        finish(2)
-        mm2(4)
+        quant_a(4)
+        add_bias(2)
         quant_a(5)
-        add_bias(4)
-        mm2(5)
+        add_bias(3)
+        copy_agg(6)
+        finish(1)
+        finish(2)
         copy_agg(7)
-        quant_a(6)
         finish(3)
-        add_bias(5)
-        mm2(6)
-        finish(4)
+        mm2(4)
+        mm2(5)
+        quant_a(6)
+        add_bias(4)
         quant_a(7)
-        add_bias(6)
-        mm2(7)
+        add_bias(5)
+        finish(4)
         finish(5)
-        add_bias(7, 0, HID // 2)
-        add_bias(7, HID // 2, HID)
+        mm2(6)
+        mm2(7)
+        add_bias(6)
+        add_bias(7, 0, 256)
+        add_bias(7, 256, 512)
         finish(6)
-        finish(7, 0, HID // 2)
-        finish(7, HID // 2, HID)
+        finish(7, 0, 256)
+        finish(7, 256, 512)

@@ -34,8 +34,8 @@ def tile_controencodnet_pa_kernel(tc, f_bytes, f_scale, x, w1, b1, out):
 
         st = {}
 
-        def bank(kind, dtype=F32, cols=512):
-            return psum.tile([P, cols], dtype, name="bank", bufs=8)
+        def bank(i, dtype=F32, cols=512):
+            return psum.tile([P, cols], dtype, name="bank%d" % i)
 
         def move(e, dst, src):
             if e == "S":
@@ -78,6 +78,7 @@ def tile_controencodnet_pa_kernel(tc, f_bytes, f_scale, x, w1, b1, out):
 
         ident = keep.tile([P, P], F32, name="ident")
         make_identity(nc, ident[:])
+        ident_bf = keep.tile([P, P], BF16, name="ident_bf")
 
         x_codes = [keep.tile([P, FEATS], U32, name="x_codes%d" % g, align_bytes=64) for g in range(NG)]
         x_scales = [keep.tile([P, FEATS], U8, name="x_scales%d" % g, align_bytes=64) for g in range(NG)]
@@ -90,15 +91,8 @@ def tile_controencodnet_pa_kernel(tc, f_bytes, f_scale, x, w1, b1, out):
                 st["c", b] = work.tile([P, NODES], BF16, name="f_bf", align_bytes=64)
             move(e, st["c", b][:, lo:hi], st["r", b][:, lo:hi].bitcast(FP8))
 
-        def spread_t(g):
-            t = bank("t")
-            col = scale[:].rearrange("p g u e -> p g (u e)")
-            for j in range(4):
-                nc.tensor.transpose(t[:, j * P : (j + 1) * P], col[:, g, j : j + 1].to_broadcast([P, P]), ident[:])
-            st["sp", g] = t
-
         def turn(b):
-            t = bank("t")
+            t = bank(b)
             words_ = st["c", b][:].bitcast(F32)
             for g in range(NG):
                 for u in range(2):
@@ -106,7 +100,7 @@ def tile_controencodnet_pa_kernel(tc, f_bytes, f_scale, x, w1, b1, out):
             st["t", b] = t
 
         def turn_h(b, g):
-            t = bank("t")
+            t = bank(b if g == 0 else NB - 1)
             words_ = st["c", b][:].bitcast(F32)
             for u in range(2):
                 nc.tensor.transpose(t[:, u * P : (u + 1) * P], words_[:, 256 * g + u : 256 * (g + 1) : 2], ident[:])
@@ -121,6 +115,11 @@ def tile_controencodnet_pa_kernel(tc, f_bytes, f_scale, x, w1, b1, out):
                 in1=scale[:, g].unsqueeze(1).to_broadcast([P, P, 2, 2]),
                 op=ALU.mult,
             )
+
+        def words_only(b):
+            w = keep.tile([P, NG, P, 2], F32, name="f_words", align_bytes=64)
+            nc.scalar.copy(out=w[:], in_=st["t", b][:].rearrange("p (u g r) -> p g r u", u=2, g=NG))
+            st["w", b] = w
 
         def mul(b):
             t = work.tile([P, NG, P, 2, 2], BF16, name="f_grp", align_bytes=64)
@@ -140,7 +139,7 @@ def tile_controencodnet_pa_kernel(tc, f_bytes, f_scale, x, w1, b1, out):
 
         def mm1(b):
             q, s = st["q", b]
-            acc = bank("a")
+            acc = bank(b)
             for t in range(4):
                 for g in range(NG):
                     nc.tensor.matmul_mx(
@@ -167,11 +166,61 @@ def tile_controencodnet_pa_kernel(tc, f_bytes, f_scale, x, w1, b1, out):
 
         def mm2(b):
             q, s = st["aq", b]
-            acc = bank("o")
+            acc = bank(b)
             nc.tensor.matmul_mx(
                 out=acc[:], lhsT=q[:].bitcast(FP8X4), lhsT_scale=s[:], rhs=w_codes[:].bitcast(FP8X4), rhs_scale=w_scales[:], start=True, stop=True
             )
             st["o", b] = acc
+
+        def bias_cols():
+            t = bank(NB - 1, BF16, 1024)
+            for j in range(4):
+                nc.tensor.transpose(t[:, j * P : (j + 1) * P], bias[:, j * P : (j + 1) * P], ident_bf[:])
+            st["bt"] = t
+
+        def bias_copy():
+            st["bc"] = keep.tile([P, 4], F32, name="bias_col")
+            nc.scalar.copy(out=st["bc"][:], in_=st["bt"][:, 0 : 4 * P : P])
+
+        def copy_agg2(b):
+            if "ag2" not in st:
+                st["ag2"] = keep.tile([P, 2, P, 4], BF16, name="a_grp2", align_bytes=64)
+            nc.scalar.copy(out=st["ag2"][:, b], in_=st["a", b][:].rearrange("p (t m) -> p m t", t=4))
+
+        def quant_a2():
+            q = keep.tile([P, 2 * P], U32, name="a_codes2", align_bytes=64)
+            s = keep.tile([P, 2 * P], U8, name="a_scales2", align_bytes=64)
+            nc.vector.quantize_mx(out=q[:].bitcast(FP8X4), scales=s[:], in_=st["ag2"][:].rearrange("p b m t -> p (b m t)"))
+            st["aq2"] = (q, s)
+
+        def mm2t(h):
+            q, s = st["aq2"]
+            acc = bank(h)
+            for j in range(2):
+                cols = slice((2 * h + j) * P, (2 * h + j + 1) * P)
+                nc.tensor.matmul_mx(
+                    out=acc[:, 256 * j : 256 * (j + 1)], lhsT=w_codes[:, cols].bitcast(FP8X4), lhsT_scale=w_scales[:, cols], rhs=q[:].bitcast(FP8X4), rhs_scale=s[:], start=True, stop=True
+                )
+            st["ot", h] = acc
+
+        def tanh_t(j):
+            t = keep.tile([P, 256], F32, name="yt%d" % j, align_bytes=64)
+            nc.scalar.activation(out=t[:], in_=st["ot", j // 2][:, 256 * (j % 2) : 256 * (j % 2 + 1)], func=ACT.Tanh, bias=st["bc"][:, j : j + 1])
+            st["yt", j] = t
+
+        def turn_back(b):
+            t = bank(b)
+            for j in range(4):
+                nc.tensor.transpose(t[:, j * P : (j + 1) * P], st["yt", j][:, b * P : (b + 1) * P], ident[:])
+            st["tb", b] = t
+
+        def store_back(b):
+            t = work.tile([P, HID], F32, name="res")
+            nc.scalar.copy(out=t[:], in_=st["tb", b][:])
+            nc.sync.dma_start(out=o_view[:, b, :], in_=t[:])
+
+        def make_ident_bf():
+            nc.vector.tensor_copy(out=ident_bf[:], in_=ident[:])
 
         def add_bias(b, lo=0, hi=HID):
             if ("p", b) not in st:
@@ -192,13 +241,16 @@ def tile_controencodnet_pa_kernel(tc, f_bytes, f_scale, x, w1, b1, out):
         def quant_x(g):
             nc.vector.quantize_mx(out=x_codes[g][:].bitcast(FP8X4), scales=x_scales[g][:], in_=x_grp[g][:].rearrange("p t m j -> p (t m j)"))
 
-        def group_w(n0, n1, e):
-            if "wg" not in st:
-                st["wg"] = keep.tile([P, 4 * HID], BF16, name="wgrp", align_bytes=64)
-            move(e, st["wg"][:].rearrange("p (n j) -> p n j", j=4)[:, n0:n1], w_raw[:].rearrange("p j n -> p n j")[:, n0:n1])
+        def group_w(h, e, after=None):
+            if after is None:
+                st["wg", h] = keep.tile([P, 2 * HID], BF16, name="wgrp", align_bytes=64)[:]
+            else:
+                st["wg", h] = st["g", after][:].rearrange("p g r u e -> p (g r u e)")
+            move(e, st["wg", h].rearrange("p (n j) -> p n j", j=4), w_raw[:, :, 256 * h : 256 * (h + 1)].rearrange("p j n -> p n j"))
 
-        def quant_w():
-            nc.vector.quantize_mx(out=w_codes[:].bitcast(FP8X4), scales=w_scales[:], in_=st["wg"][:])
+        def quant_w(h):
+            cols = slice(256 * h, 256 * (h + 1))
+            nc.vector.quantize_mx(out=w_codes[:, cols].bitcast(FP8X4), scales=w_scales[:, cols], in_=st["wg", h])
 
         load_f(0, 1)
         load_f(1, 2)
@@ -207,25 +259,24 @@ def tile_controencodnet_pa_kernel(tc, f_bytes, f_scale, x, w1, b1, out):
         load_x(1)
         load_f(4, 6)
         load_f(6, 8)
-        load_w()
         load_b()
+        load_w()
+        make_ident_bf()
         cast(0, "V", 0, 512)
         cast(0, "S", 512, 1024)
         cast(1, "S")
         cast(2, "S")
         cast(3, "S")
         group_x(0, 64, 128, "S")
-        cast(4, "S")
         group_x(1, 48, 128, "S")
+        cast(4, "S")
         cast(5, "S")
-        cast(6, "S")
-        cast(7, "S")
-        group_w(0, 512, "S")
         turn_h(0,0)
         turn_h(0,1)
         turn(1)
         turn(2)
         turn(3)
+        bias_cols()
         turn(4)
         turn(5)
         group_x(0, 0, 64, "G")
@@ -237,68 +288,77 @@ def tile_controencodnet_pa_kernel(tc, f_bytes, f_scale, x, w1, b1, out):
         mul(3)
         quant_x(0)
         quant_f(0)
-        quant_f(1)
         quant_x(1)
+        quant_f(1)
         quant_f(2)
         quant_f(3)
         mul(4)
         mul(5)
         quant_f(4)
-        quant_w()
-        mm1(0)
+        bias_copy()
+        cast(6, "S")
+        cast(7, "S")
+        group_w(0,"S")
         turn(6)
-        turn(7)
+        mm1(0)
         mm1(1)
         mm1(2)
         mm1(3)
-        copy_agg(0)
-        copy_agg(1)
+        mm1(4)
+        group_w(1,"G",3)
+        quant_w(0)
+        quant_w(1)
+        copy_agg2(0)
+        copy_agg2(1)
         copy_agg(2)
         copy_agg(3)
-        quant_a(0)
-        mul(6)
+        copy_agg(4)
+        quant_a2()
         quant_f(5)
-        quant_a(1)
         quant_a(2)
-        mm2(0)
-        mm1(4)
-        mm2(1)
+        mul(6)
+        quant_a(3)
+        mm2t(0)
+        mm2t(1)
+        mm2(2)
         mm1(5)
-        add_bias(0)
+        turn(7)
+        add_bias(2)
+        quant_a(4)
         quant_f(6)
         mul(7)
-        quant_a(3)
-        add_bias(1)
-        quant_f(7)
-        copy_agg(4)
-        finish(0)
+        tanh_t(0)
+        tanh_t(1)
+        tanh_t(2)
+        tanh_t(3)
         copy_agg(5)
-        mm1(6)
-        mm2(2)
-        mm2(3)
-        mm1(7)
-        quant_a(4)
-        add_bias(2)
-        quant_a(5)
-        add_bias(3)
-        copy_agg(6)
-        finish(1)
         finish(2)
-        copy_agg(7)
-        finish(3)
+        turn_back(0)
+        turn_back(1)
+        mm1(6)
+        mm2(3)
         mm2(4)
+        quant_a(5)
+        quant_f(7)
+        add_bias(3)
+        store_back(0)
+        copy_agg(6)
+        store_back(1)
+        finish(3)
         mm2(5)
+        mm1(7)
         quant_a(6)
         add_bias(4)
-        quant_a(7)
         add_bias(5)
+        copy_agg(7)
         finish(4)
         finish(5)
         mm2(6)
-        mm2(7)
         add_bias(6)
+        quant_a(7)
+        finish(6)
+        mm2(7)
         add_bias(7, 0, 256)
         add_bias(7, 256, 512)
-        finish(6)
         finish(7, 0, 256)
         finish(7, 256, 512)

@@ -172,15 +172,21 @@ def tile_controencodnet_pa_kernel(tc, f_bytes, f_scale, x, w1, b1, out):
             )
             st["o", b] = acc
 
+        def zero_rows():
+            st["br"] = keep.tile([P, P], BF16, name="bias_rows")
+            nc.vector.memset(st["br"][:], 0.0)
+
+        def load_rows():
+            nc.sync.dma_start(out=st["br"][0:4, :], in_=b1.rearrange("(j p) -> j p", j=4))
+
         def bias_cols():
             t = bank(NB - 1, BF16, 1024)
-            for j in range(4):
-                nc.tensor.transpose(t[:, j * P : (j + 1) * P], bias[:, j * P : (j + 1) * P], ident_bf[:])
+            nc.tensor.transpose(t[:, 0:P], st["br"][:], ident_bf[:])
             st["bt"] = t
 
         def bias_copy():
             st["bc"] = keep.tile([P, 4], F32, name="bias_col")
-            nc.scalar.copy(out=st["bc"][:], in_=st["bt"][:, 0 : 4 * P : P])
+            nc.scalar.copy(out=st["bc"][:], in_=st["bt"][:, 0:4])
 
         def copy_agg2(b):
             if "ag2" not in st:
@@ -252,15 +258,17 @@ def tile_controencodnet_pa_kernel(tc, f_bytes, f_scale, x, w1, b1, out):
             cols = slice(256 * h, 256 * (h + 1))
             nc.vector.quantize_mx(out=w_codes[:, cols].bitcast(FP8X4), scales=w_scales[:, cols], in_=st["wg", h])
 
+        zero_rows()
         load_f(0, 1)
         load_f(1, 2)
         load_f(2, 4)
         load_x(0)
         load_x(1)
         load_f(4, 6)
+        load_rows()
         load_f(6, 8)
-        load_b()
         load_w()
+        load_b()
         make_ident_bf()
         cast(0, "V", 0, 512)
         cast(0, "S", 512, 1024)

@@ -16,357 +16,316 @@ ACT = mybir.ActivationFunctionType
 ALU = mybir.AluOpType
 
 P = 128
-NB = 8
-NG = 2
+PACK = 4
+BLOCKS = NODES // P
+PASSES = NODES // (P * PACK)
+K_PASS = P * PACK
+RUN = 8
+PAIR = 2
+HALF = HID // 2
+LAST = BLOCKS - 1
+
+X_COLS_ON_GPSIMD = 352
+W_COLS_ON_GPSIMD = 160
 
 
 def tile_controencodnet_pa_kernel(tc, f_bytes, f_scale, x, w1, b1, out):
     nc = tc.nc
-    f_view = f_bytes.rearrange("(p b) k -> p b k", b=NB)
-    o_view = out.rearrange("(p b) h -> p b h", b=NB)
-    x_view = x.rearrange("(g p j) n -> g p j n", p=P, j=4)
+    f_view = f_bytes.rearrange("(r b) k -> r b k", b=BLOCKS)
+    out_view = out.rearrange("(r b) h -> r b h", b=BLOCKS)
+    x_view = x.rearrange("(g p t) c -> g p t c", p=P, t=PACK)
+    w_view = w1.rearrange("(a t i) h -> t a i h", t=PACK, i=RUN)
 
     with ExitStack() as ctx:
         keep = ctx.enter_context(tc.tile_pool(name="keep", bufs=1))
-        work = ctx.enter_context(tc.tile_pool(name="work", bufs=NB))
+        each = ctx.enter_context(tc.tile_pool(name="each", bufs=BLOCKS))
         psum = ctx.enter_context(tc.psum_pool(name="psum", bufs=1))
         ctx.enter_context(tc.manual_schedule())
 
-        st = {}
+        def bank(number, dtype=F32, columns=512):
+            return psum.tile([P, columns], dtype, name="bank%d" % number)
 
-        def bank(i, dtype=F32, cols=512):
-            return psum.tile([P, cols], dtype, name="bank%d" % i)
+        def gpsimd_copy(dst, src):
+            nc.gpsimd.tensor_scalar(out=dst, in0=src, scalar1=1.0, scalar2=0.0, op0=ALU.mult, op1=ALU.add)
 
-        def move(e, dst, src):
-            if e == "S":
-                nc.scalar.copy(out=dst, in_=src)
-            elif e == "V":
-                nc.vector.tensor_copy(out=dst, in_=src)
-            else:
-                nc.gpsimd.tensor_scalar(out=dst, in0=src, scalar1=1.0, scalar2=0.0, op0=ALU.mult, op1=ALU.add)
+        scale = keep.tile([P, PASSES, PACK], F32, name="scale")
+        nc.scalar.dma_start(out=scale[:], in_=f_scale.rearrange("o (g p t) -> p (o g) t", p=P, t=PACK))
 
-        scale = keep.tile([P, NG, 2, 2], F32, name="scale")
-        nc.scalar.dma_start(
-            out=scale[:].rearrange("p g u e -> p g (u e)"),
-            in_=f_scale.rearrange("o (g p t) -> p (o g) t", p=P, t=4),
-        )
-        dummy = keep.tile([P, 1], F32, name="dummy")
-        dummy2 = keep.tile([P, 1], F32, name="dummy2")
-        nc.vector.memset(dummy[:], 0.0)
-        nc.scalar.activation(out=dummy2[:], in_=dummy[:], func=ACT.Tanh)
+        table_in = keep.tile([P, 1], F32, name="table_in")
+        table_out = keep.tile([P, 1], F32, name="table_out")
+        nc.vector.memset(table_in[:], 0.0)
+        nc.scalar.activation(out=table_out[:], in_=table_in[:], func=ACT.Tanh)
 
-        def load_f(b0, b1_):
-            t = keep.tile([P, b1_ - b0, NODES], U8, name="raw%d" % b0)
-            nc.sync.dma_start(out=t[:], in_=f_view[:, b0:b1_, :])
-            for b in range(b0, b1_):
-                st["r", b] = t[:, b - b0, :]
+        identity = keep.tile([P, P], F32, name="identity")
+        make_identity(nc, identity[:])
 
-        x_raw = [keep.tile([P, 4, FEATS], BF16, name="x_raw%d" % g) for g in range(NG)]
-        w_raw = keep.tile([P, 4, HID], BF16, name="w_raw")
+        bias_rows = keep.tile([P, P], BF16, name="bias_rows")
+        nc.vector.memset(bias_rows[:], 0.0)
+
+        raw = {}
+
+        def load_f(first, count):
+            tile = keep.tile([P, count, NODES], U8, name="f_raw%d" % first)
+            nc.sync.dma_start(out=tile[:], in_=f_view[:, first : first + count, :])
+            for j in range(count):
+                raw[first + j] = tile[:, j, :]
+
+        x_raw = [keep.tile([P, PACK, FEATS], BF16, name="x_raw%d" % g) for g in range(PASSES)]
+        w_raw = keep.tile([P, PACK, HID], BF16, name="w_raw")
         bias = keep.tile([P, HID], BF16, name="bias")
 
-        def load_x(g):
-            nc.sync.dma_start(out=x_raw[g][:], in_=x_view[g])
+        load_f(0, 1)
+        load_f(1, 1)
+        load_f(2, 2)
+        nc.sync.dma_start(out=x_raw[0][:], in_=x_view[0])
+        load_f(4, 2)
+        nc.sync.dma_start(out=x_raw[1][:], in_=x_view[1])
+        nc.sync.dma_start(out=bias_rows[0 : HID // P, :], in_=b1.rearrange("(j p) -> j p", p=P))
+        load_f(6, 2)
+        for t in range(PACK):
+            nc.sync.dma_start(out=w_raw[:, t, :], in_=w_view[t])
+        nc.sync.dma_start(out=bias[:], in_=b1.partition_broadcast(P))
 
-        def load_w():
-            rows = w1.rearrange("(a t i) n -> t a i n", t=4, i=8)
-            for t in range(4):
-                nc.sync.dma_start(out=w_raw[:, t, :], in_=rows[t])
+        identity_bf = keep.tile([P, P], BF16, name="identity_bf")
+        nc.vector.tensor_copy(out=identity_bf[:], in_=identity[:])
 
-        def load_b():
-            nc.sync.dma_start(out=bias[:], in_=b1.partition_broadcast(P))
-
-        ident = keep.tile([P, P], F32, name="ident")
-        make_identity(nc, ident[:])
-        ident_bf = keep.tile([P, P], BF16, name="ident_bf")
-
-        x_codes = [keep.tile([P, FEATS], U32, name="x_codes%d" % g, align_bytes=64) for g in range(NG)]
-        x_scales = [keep.tile([P, FEATS], U8, name="x_scales%d" % g, align_bytes=64) for g in range(NG)]
-        x_grp = [keep.tile([P, 4, P, 4], BF16, name="grp", align_bytes=64, bufs=2) for g in range(NG)]
+        x_grouped = [keep.tile([P, PACK, P, PACK], BF16, name="x_grouped%d" % g, align_bytes=64) for g in range(PASSES)]
+        x_codes = [keep.tile([P, FEATS], U32, name="x_codes%d" % g, align_bytes=64) for g in range(PASSES)]
+        x_scales = [keep.tile([P, FEATS], U8, name="x_scales%d" % g, align_bytes=64) for g in range(PASSES)]
         w_codes = keep.tile([P, HID], U32, name="w_codes", align_bytes=64)
         w_scales = keep.tile([P, HID], U8, name="w_scales", align_bytes=64)
 
-        def cast(b, e, lo=0, hi=NODES):
-            if ("c", b) not in st:
-                st["c", b] = work.tile([P, NODES], BF16, name="f_bf", align_bytes=64)
-            move(e, st["c", b][:, lo:hi], st["r", b][:, lo:hi].bitcast(FP8))
+        wide, turned, scaled, f_mx, agg, agg_grouped, agg_mx, second, biased, result = ({} for unused in range(10))
+
+        def widen(b):
+            wide[b] = each.tile([P, NODES], BF16, name="wide", align_bytes=64)
+            nc.scalar.copy(out=wide[b][:], in_=raw[b].bitcast(FP8))
+
+        def turn_pass(dst, b, g):
+            words = wide[b][:].bitcast(F32)
+            for u in range(2):
+                nc.tensor.transpose(dst(u), words[:, 2 * P * g + u : 2 * P * (g + 1) : 2], identity[:])
 
         def turn(b):
-            t = bank(b)
-            words_ = st["c", b][:].bitcast(F32)
-            for g in range(NG):
-                for u in range(2):
-                    nc.tensor.transpose(t[:, (2 * u + g) * P : (2 * u + g + 1) * P], words_[:, 256 * g + u : 256 * (g + 1) : 2], ident[:])
-            st["t", b] = t
+            turned[b] = bank(b)
+            view = turned[b][:].rearrange("p (u g r) -> p u g r", u=2, g=PASSES)
+            for g in range(PASSES):
+                turn_pass(lambda u: view[:, u, g, :], b, g)
 
-        def turn_h(b, g):
-            t = bank(b if g == 0 else NB - 1)
-            words_ = st["c", b][:].bitcast(F32)
-            for u in range(2):
-                nc.tensor.transpose(t[:, u * P : (u + 1) * P], words_[:, 256 * g + u : 256 * (g + 1) : 2], ident[:])
-            st["th", b, g] = t
-
-        def mul_h(b, g):
-            if ("g", b) not in st:
-                st["g", b] = work.tile([P, NG, P, 2, 2], BF16, name="f_grp", align_bytes=64)
+        def scale_out(b):
+            scaled[b] = each.tile([P, PASSES, P, 2, 2], BF16, name="scaled", align_bytes=64)
             nc.vector.tensor_tensor(
-                out=st["g", b][:, g],
-                in0=st["th", b, g][:, 0 : 2 * P].bitcast(BF16).rearrange("p (u r e) -> p r u e", u=2, e=2),
-                in1=scale[:, g].unsqueeze(1).to_broadcast([P, P, 2, 2]),
+                out=scaled[b][:],
+                in0=turned[b][:].bitcast(BF16).rearrange("p (u g r e) -> p g r u e", u=2, g=PASSES, e=2),
+                in1=scale[:].rearrange("p g (u e) -> p g u e", e=2).unsqueeze(2).to_broadcast([P, PASSES, P, 2, 2]),
                 op=ALU.mult,
             )
 
-        def words_only(b):
-            w = keep.tile([P, NG, P, 2], F32, name="f_words", align_bytes=64)
-            nc.scalar.copy(out=w[:], in_=st["t", b][:].rearrange("p (u g r) -> p g r u", u=2, g=NG))
-            st["w", b] = w
-
-        def mul(b):
-            t = work.tile([P, NG, P, 2, 2], BF16, name="f_grp", align_bytes=64)
-            nc.vector.tensor_tensor(
-                out=t[:],
-                in0=st["t", b][:].bitcast(BF16).rearrange("p (u g r e) -> p g r u e", u=2, g=NG, e=2),
-                in1=scale[:].unsqueeze(2).to_broadcast([P, NG, P, 2, 2]),
-                op=ALU.mult,
-            )
-            st["g", b] = t
-
-        def quant_f(b):
-            q = work.tile([P, NG * P], U32, name="f_codes", align_bytes=64)
-            s = work.tile([P, NG * P], U8, name="f_scales", align_bytes=64)
-            nc.vector.quantize_mx(out=q[:].bitcast(FP8X4), scales=s[:], in_=st["g", b][:].rearrange("p g r u e -> p (g r u e)"))
-            st["q", b] = (q, s)
-
-        def mm1(b):
-            q, s = st["q", b]
-            acc = bank(b)
-            for t in range(4):
-                for g in range(NG):
-                    nc.tensor.matmul_mx(
-                        out=acc[:, t * P : (t + 1) * P],
-                        lhsT=x_codes[g][:, t * P : (t + 1) * P].bitcast(FP8X4),
-                        lhsT_scale=x_scales[g][:, t * P : (t + 1) * P],
-                        rhs=q[:, g * P : (g + 1) * P].bitcast(FP8X4),
-                        rhs_scale=s[:, g * P : (g + 1) * P],
-                        start=(g == 0),
-                        stop=(g == NG - 1),
-                    )
-            st["a", b] = acc
-
-        def copy_agg(b, e="S"):
-            t = work.tile([P, P, 4], BF16, name="a_grp", align_bytes=64)
-            move(e, t[:], st["a", b][:].rearrange("p (t m) -> p m t", t=4))
-            st["ag", b] = t
-
-        def quant_a(b):
-            q = work.tile([P, P], U32, name="a_codes", align_bytes=64)
-            s = work.tile([P, P], U8, name="a_scales", align_bytes=64)
-            nc.vector.quantize_mx(out=q[:].bitcast(FP8X4), scales=s[:], in_=st["ag", b][:].rearrange("p m t -> p (m t)"))
-            st["aq", b] = (q, s)
-
-        def mm2(b):
-            q, s = st["aq", b]
-            acc = bank(b)
-            nc.tensor.matmul_mx(
-                out=acc[:], lhsT=q[:].bitcast(FP8X4), lhsT_scale=s[:], rhs=w_codes[:].bitcast(FP8X4), rhs_scale=w_scales[:], start=True, stop=True
-            )
-            st["o", b] = acc
-
-        def zero_rows():
-            st["br"] = keep.tile([P, P], BF16, name="bias_rows")
-            nc.vector.memset(st["br"][:], 0.0)
-
-        def load_rows():
-            nc.sync.dma_start(out=st["br"][0:4, :], in_=b1.rearrange("(j p) -> j p", j=4))
-
-        def bias_cols():
-            t = bank(NB - 1, BF16, 1024)
-            nc.tensor.transpose(t[:, 0:P], st["br"][:], ident_bf[:])
-            st["bt"] = t
-
-        def bias_copy():
-            st["bc"] = keep.tile([P, 4], F32, name="bias_col")
-            nc.scalar.copy(out=st["bc"][:], in_=st["bt"][:, 0:4])
-
-        def copy_agg2(b):
-            if "ag2" not in st:
-                st["ag2"] = keep.tile([P, 2, P, 4], BF16, name="a_grp2", align_bytes=64)
-            nc.scalar.copy(out=st["ag2"][:, b], in_=st["a", b][:].rearrange("p (t m) -> p m t", t=4))
-
-        def quant_a2():
-            q = keep.tile([P, 2 * P], U32, name="a_codes2", align_bytes=64)
-            s = keep.tile([P, 2 * P], U8, name="a_scales2", align_bytes=64)
-            nc.vector.quantize_mx(out=q[:].bitcast(FP8X4), scales=s[:], in_=st["ag2"][:].rearrange("p b m t -> p (b m t)"))
-            st["aq2"] = (q, s)
-
-        def mm2t(h):
-            q, s = st["aq2"]
-            acc = bank(h)
-            for j in range(2):
-                cols = slice((2 * h + j) * P, (2 * h + j + 1) * P)
-                nc.tensor.matmul_mx(
-                    out=acc[:, 256 * j : 256 * (j + 1)], lhsT=w_codes[:, cols].bitcast(FP8X4), lhsT_scale=w_scales[:, cols], rhs=q[:].bitcast(FP8X4), rhs_scale=s[:], start=True, stop=True
+        def first_block():
+            wide[0] = each.tile([P, NODES], BF16, name="wide", align_bytes=64)
+            nc.vector.tensor_copy(out=wide[0][:, :K_PASS], in_=raw[0][:, :K_PASS].bitcast(FP8))
+            nc.scalar.copy(out=wide[0][:, K_PASS:], in_=raw[0][:, K_PASS:].bitcast(FP8))
+            scaled[0] = each.tile([P, PASSES, P, 2, 2], BF16, name="scaled", align_bytes=64)
+            for g, number in enumerate((0, LAST)):
+                half = bank(number)
+                turn_pass(lambda u: half[:, u * P : (u + 1) * P], 0, g)
+                nc.vector.tensor_tensor(
+                    out=scaled[0][:, g],
+                    in0=half[:, : 2 * P].bitcast(BF16).rearrange("p (u r e) -> p r u e", u=2, e=2),
+                    in1=scale[:, g].rearrange("p (u e) -> p u e", e=2).unsqueeze(1).to_broadcast([P, P, 2, 2]),
+                    op=ALU.mult,
                 )
-            st["ot", h] = acc
 
-        def tanh_t(j):
-            t = keep.tile([P, 256], F32, name="yt%d" % j, align_bytes=64)
-            nc.scalar.activation(out=t[:], in_=st["ot", j // 2][:, 256 * (j % 2) : 256 * (j % 2 + 1)], func=ACT.Tanh, bias=st["bc"][:, j : j + 1])
-            st["yt", j] = t
+        def quantize_f(b):
+            codes = each.tile([P, PASSES * P], U32, name="f_codes", align_bytes=64)
+            scales = each.tile([P, PASSES * P], U8, name="f_scales", align_bytes=64)
+            nc.vector.quantize_mx(out=codes[:].bitcast(FP8X4), scales=scales[:], in_=scaled[b][:].rearrange("p g r u e -> p (g r u e)"))
+            f_mx[b] = (codes, scales)
+
+        def group_x(copy, g, first, end):
+            runs = slice(first // (PACK * RUN), end // (PACK * RUN))
+            dst = x_grouped[g][:].rearrange("p s (a i) t -> p a s i t", i=RUN)[:, runs]
+            copy(dst, x_raw[g][:].rearrange("p t (a s i) -> p a s i t", s=PACK, i=RUN)[:, runs])
+
+        def quantize_x(g):
+            nc.vector.quantize_mx(out=x_codes[g][:].bitcast(FP8X4), scales=x_scales[g][:], in_=x_grouped[g][:].rearrange("p s m t -> p (s m t)"))
+
+        def group_w(copy, grouped, half, first, end):
+            src = w_raw[:, :, HALF * half + first : HALF * half + end].rearrange("p t h -> p h t")
+            copy(grouped.rearrange("p (h t) -> p h t", t=PACK)[:, first:end], src)
+
+        def quantize_w(grouped, half):
+            cols = slice(HALF * half, HALF * (half + 1))
+            nc.vector.quantize_mx(out=w_codes[:, cols].bitcast(FP8X4), scales=w_scales[:, cols], in_=grouped)
+
+        def first_product(b):
+            codes, scales = f_mx[b]
+            agg[b] = bank(b)
+            for s in range(PACK):
+                cols = slice(s * P, (s + 1) * P)
+                for g in range(PASSES):
+                    nodes = slice(g * P, (g + 1) * P)
+                    nc.tensor.matmul_mx(
+                        out=agg[b][:, cols],
+                        lhsT=x_codes[g][:, cols].bitcast(FP8X4),
+                        lhsT_scale=x_scales[g][:, cols],
+                        rhs=codes[:, nodes].bitcast(FP8X4),
+                        rhs_scale=scales[:, nodes],
+                        start=(g == 0),
+                        stop=(g == PASSES - 1),
+                    )
+
+        pair_grouped = keep.tile([P, PAIR, P, PACK], BF16, name="pair_grouped", align_bytes=64)
+
+        def copy_agg(b):
+            if b < PAIR:
+                agg_grouped[b] = pair_grouped[:, b]
+            else:
+                agg_grouped[b] = each.tile([P, P, PACK], BF16, name="agg_grouped", align_bytes=64)[:]
+            nc.scalar.copy(out=agg_grouped[b], in_=agg[b][:].rearrange("p (s r) -> p r s", s=PACK))
+
+        def quantize_agg(b):
+            codes = each.tile([P, P], U32, name="agg_codes", align_bytes=64)
+            scales = each.tile([P, P], U8, name="agg_scales", align_bytes=64)
+            nc.vector.quantize_mx(out=codes[:].bitcast(FP8X4), scales=scales[:], in_=agg_grouped[b].rearrange("p r s -> p (r s)"))
+            agg_mx[b] = (codes, scales)
+
+        def second_product(b):
+            codes, scales = agg_mx[b]
+            second[b] = bank(b)
+            nc.tensor.matmul_mx(
+                out=second[b][:],
+                lhsT=codes[:].bitcast(FP8X4),
+                lhsT_scale=scales[:],
+                rhs=w_codes[:].bitcast(FP8X4),
+                rhs_scale=w_scales[:],
+                start=True,
+                stop=True,
+            )
+
+        def add_bias(b, cols=slice(0, HID)):
+            if b not in biased:
+                biased[b] = each.tile([P, HID], F32, name="biased")
+            nc.vector.tensor_tensor(out=biased[b][:, cols], in0=second[b][:, cols], in1=bias[:, cols], op=ALU.add)
+
+        def finish(b, cols=slice(0, HID)):
+            if b not in result:
+                result[b] = each.tile([P, HID], F32, name="result")
+            nc.scalar.activation(out=result[b][:, cols], in_=biased[b][:, cols], func=ACT.Tanh)
+            nc.sync.dma_start(out=out_view[:, b, cols], in_=result[b][:, cols])
+
+        pair_tanh = [keep.tile([P, PAIR * P], F32, name="pair_tanh%d" % j, align_bytes=64) for j in range(HID // P)]
+
+        def pair_product(bias_columns):
+            codes = keep.tile([P, PAIR * P], U32, name="pair_codes", align_bytes=64)
+            scales = keep.tile([P, PAIR * P], U8, name="pair_scales", align_bytes=64)
+            nc.vector.quantize_mx(out=codes[:].bitcast(FP8X4), scales=scales[:], in_=pair_grouped[:].rearrange("p b r s -> p (b r s)"))
+            banks = [bank(number) for number in range(PAIR)]
+            tiles = [banks[j // 2][:, (j % 2) * PAIR * P : (j % 2 + 1) * PAIR * P] for j in range(HID // P)]
+            for j, tile in enumerate(tiles):
+                cols = slice(j * P, (j + 1) * P)
+                nc.tensor.matmul_mx(
+                    out=tile,
+                    lhsT=w_codes[:, cols].bitcast(FP8X4),
+                    lhsT_scale=w_scales[:, cols],
+                    rhs=codes[:].bitcast(FP8X4),
+                    rhs_scale=scales[:],
+                    start=True,
+                    stop=True,
+                )
+            for j, tile in enumerate(tiles):
+                nc.scalar.activation(out=pair_tanh[j][:], in_=tile, func=ACT.Tanh, bias=bias_columns[:, j : j + 1])
 
         def turn_back(b):
-            t = bank(b)
-            for j in range(4):
-                nc.tensor.transpose(t[:, j * P : (j + 1) * P], st["yt", j][:, b * P : (b + 1) * P], ident[:])
-            st["tb", b] = t
+            second[b] = bank(b)
+            for j in range(HID // P):
+                nc.tensor.transpose(second[b][:, j * P : (j + 1) * P], pair_tanh[j][:, b * P : (b + 1) * P], identity[:])
 
-        def store_back(b):
-            t = work.tile([P, HID], F32, name="res")
-            nc.scalar.copy(out=t[:], in_=st["tb", b][:])
-            nc.sync.dma_start(out=o_view[:, b, :], in_=t[:])
+        def store_turned(b):
+            result[b] = each.tile([P, HID], F32, name="result")
+            nc.scalar.copy(out=result[b][:], in_=second[b][:])
+            nc.sync.dma_start(out=out_view[:, b, :], in_=result[b][:])
 
-        def make_ident_bf():
-            nc.vector.tensor_copy(out=ident_bf[:], in_=ident[:])
+        def scalar_copy(dst, src):
+            nc.scalar.copy(out=dst, in_=src)
 
-        def add_bias(b, lo=0, hi=HID):
-            if ("p", b) not in st:
-                st["p", b] = work.tile([P, HID], F32, name="pre")
-            nc.vector.tensor_tensor(out=st["p", b][:, lo:hi], in0=st["o", b][:, lo:hi], in1=bias[:, lo:hi], op=ALU.add)
+        first_block()
+        for b in range(1, 4):
+            widen(b)
+            turn(b)
+            scale_out(b)
+        group_x(gpsimd_copy, 0, 0, X_COLS_ON_GPSIMD)
+        group_x(scalar_copy, 0, X_COLS_ON_GPSIMD, FEATS)
+        for b in (4, 5):
+            widen(b)
+            turn(b)
+        group_x(scalar_copy, 1, 0, FEATS)
 
-        def finish(b, lo=0, hi=HID):
-            if ("y", b) not in st:
-                st["y", b] = work.tile([P, HID], F32, name="res")
-            t = st["y", b]
-            nc.scalar.activation(out=t[:, lo:hi], in_=st["p", b][:, lo:hi], func=ACT.Tanh)
-            nc.sync.dma_start(out=o_view[:, b, lo:hi], in_=t[:, lo:hi])
-
-        def group_x(g, m0, m1, e):
-            dst = x_grp[g][:].rearrange("p t (a i) j -> p a t i j", i=8)[:, m0 // 8 : m1 // 8]
-            move(e, dst, x_raw[g][:].rearrange("p j (a t i) -> p a t i j", t=4, i=8)[:, m0 // 8 : m1 // 8])
-
-        def quant_x(g):
-            nc.vector.quantize_mx(out=x_codes[g][:].bitcast(FP8X4), scales=x_scales[g][:], in_=x_grp[g][:].rearrange("p t m j -> p (t m j)"))
-
-        def group_w(h, e, after=None):
-            if after is None:
-                st["wg", h] = keep.tile([P, 2 * HID], BF16, name="wgrp", align_bytes=64)[:]
-            else:
-                st["wg", h] = st["g", after][:].rearrange("p g r u e -> p (g r u e)")
-            move(e, st["wg", h].rearrange("p (n j) -> p n j", j=4), w_raw[:, :, 256 * h : 256 * (h + 1)].rearrange("p j n -> p n j"))
-
-        def quant_w(h):
-            cols = slice(256 * h, 256 * (h + 1))
-            nc.vector.quantize_mx(out=w_codes[:, cols].bitcast(FP8X4), scales=w_scales[:, cols], in_=st["wg", h])
-
-        zero_rows()
-        load_f(0, 1)
-        load_f(1, 2)
-        load_f(2, 4)
-        load_x(0)
-        load_x(1)
-        load_f(4, 6)
-        load_rows()
-        load_f(6, 8)
-        load_w()
-        load_b()
-        make_ident_bf()
-        cast(0, "V", 0, 512)
-        cast(0, "S", 512, 1024)
-        cast(1, "S")
-        cast(2, "S")
-        cast(3, "S")
-        group_x(0, 64, 128, "S")
-        group_x(1, 48, 128, "S")
-        cast(4, "S")
-        cast(5, "S")
-        turn_h(0,0)
-        turn_h(0,1)
-        turn(1)
-        turn(2)
-        turn(3)
-        bias_cols()
-        turn(4)
-        turn(5)
-        group_x(0, 0, 64, "G")
-        group_x(1, 0, 48, "G")
-        mul_h(0,0)
-        mul_h(0,1)
-        mul(1)
-        mul(2)
-        mul(3)
-        quant_x(0)
-        quant_f(0)
-        quant_x(1)
-        quant_f(1)
-        quant_f(2)
-        quant_f(3)
-        mul(4)
-        mul(5)
-        quant_f(4)
-        bias_copy()
-        cast(6, "S")
-        cast(7, "S")
-        group_w(0,"S")
+        bias_turned = bank(2, BF16, 2 * 512)
+        nc.tensor.transpose(bias_turned[:, :P], bias_rows[:], identity_bf[:])
+        widen(6)
+        bias_columns = keep.tile([P, HID // P], F32, name="bias_columns")
+        nc.scalar.copy(out=bias_columns[:], in_=bias_turned[:, : HID // P])
         turn(6)
-        mm1(0)
-        mm1(1)
-        mm1(2)
-        mm1(3)
-        mm1(4)
-        group_w(1,"G",3)
-        quant_w(0)
-        quant_w(1)
-        copy_agg2(0)
-        copy_agg2(1)
-        copy_agg(2)
-        copy_agg(3)
-        copy_agg(4)
-        quant_a2()
-        quant_f(5)
-        quant_a(2)
-        mul(6)
-        quant_a(3)
-        mm2t(0)
-        mm2t(1)
-        mm2(2)
-        mm1(5)
-        turn(7)
+
+        quantize_x(0)
+        for b in range(3):
+            quantize_f(b)
+        quantize_x(1)
+        quantize_f(3)
+
+        w_grouped = [keep.tile([P, PACK * HALF], BF16, name="w_grouped", align_bytes=64)[:], scaled[3][:].rearrange("p g r u e -> p (g r u e)")]
+        group_w(scalar_copy, w_grouped[0], 0, 0, HALF)
+        widen(LAST)
+        group_w(gpsimd_copy, w_grouped[1], 1, 0, W_COLS_ON_GPSIMD)
+        group_w(scalar_copy, w_grouped[1], 1, W_COLS_ON_GPSIMD, HALF)
+        scale_out(4)
+        scale_out(5)
+        quantize_f(4)
+        for b in range(5):
+            first_product(b)
+            copy_agg(b)
+        for half in range(2):
+            quantize_w(w_grouped[half], half)
+        pair_product(bias_columns)
+
+        quantize_f(5)
+        quantize_agg(2)
+        second_product(2)
+        first_product(5)
+        turn(LAST)
+        scale_out(6)
+        quantize_agg(3)
         add_bias(2)
-        quant_a(4)
-        quant_f(6)
-        mul(7)
-        tanh_t(0)
-        tanh_t(1)
-        tanh_t(2)
-        tanh_t(3)
+        quantize_agg(4)
+        quantize_f(6)
         copy_agg(5)
         finish(2)
-        turn_back(0)
-        turn_back(1)
-        mm1(6)
-        mm2(3)
-        mm2(4)
-        quant_a(5)
-        quant_f(7)
-        add_bias(3)
-        store_back(0)
+        for b in range(PAIR):
+            turn_back(b)
+        store_turned(0)
+        first_product(6)
         copy_agg(6)
-        store_back(1)
+        store_turned(1)
+        scale_out(LAST)
+        quantize_agg(5)
+        quantize_f(LAST)
+
+        for b in range(3, 6):
+            second_product(b)
+        first_product(LAST)
+        add_bias(3)
         finish(3)
-        mm2(5)
-        mm1(7)
-        quant_a(6)
-        add_bias(4)
-        add_bias(5)
-        copy_agg(7)
-        finish(4)
-        finish(5)
-        mm2(6)
-        add_bias(6)
-        quant_a(7)
-        finish(6)
-        mm2(7)
-        add_bias(7, 0, 256)
-        add_bias(7, 256, 512)
-        finish(7, 0, 256)
-        finish(7, 256, 512)
+        quantize_agg(6)
+        second_product(6)
+        copy_agg(LAST)
+        for b in range(4, LAST):
+            add_bias(b)
+            finish(b)
+
+        quantize_agg(LAST)
+        second_product(LAST)
+        for half in range(2):
+            cols = slice(HALF * half, HALF * (half + 1))
+            add_bias(LAST, cols)
+            finish(LAST, cols)

@@ -263,6 +263,11 @@ def tile_controencodnet_pa_kernel(tc, f_bytes, f_scale, x, w1, b1, out):
 
         bias_turned = bank(2, BF16, 2 * 512)
         nc.tensor.transpose(bias_turned[:, :P], bias_rows[:], identity_bf[:])
+
+        warm = bank(1)
+        for unused in range(4):
+            nc.tensor.matmul(out=warm[:], lhsT=identity_bf[:], rhs=wide[1][:, :512], start=True, stop=True)
+
         widen(6)
         bias_columns = keep.tile([P, HID // P], F32, name="bias_columns")
         nc.scalar.copy(out=bias_columns[:], in_=bias_turned[:, : HID // P])

@@ -25,8 +25,8 @@ PAIR = 2
 HALF = HID // 2
 LAST = BLOCKS - 1
 
-X_COLS_ON_GPSIMD = 352
-W_COLS_ON_GPSIMD = 160
+X_COLS_ON_GPSIMD = 416
+W_COLS_ON_GPSIMD = 192
 
 
 def tile_controencodnet_pa_kernel(tc, f_bytes, f_scale, x, w1, b1, out):

@@ -25,8 +25,8 @@ PAIR = 2
 HALF = HID // 2
 LAST = BLOCKS - 1
 
-X_COLS_ON_GPSIMD = 416
-W_COLS_ON_GPSIMD = 192
+GROUPS = [(0, 1)]
+SPLIT = 256
 
 
 def tile_controencodnet_pa_kernel(tc, f_bytes, f_scale, x, w1, b1, out):
@@ -49,7 +49,6 @@ def tile_controencodnet_pa_kernel(tc, f_bytes, f_scale, x, w1, b1, out):
             nc.gpsimd.tensor_scalar(out=dst, in0=src, scalar1=1.0, scalar2=0.0, op0=ALU.mult, op1=ALU.add)
 
         scale = keep.tile([P, PASSES, PACK], F32, name="scale")
-        nc.scalar.dma_start(out=scale[:], in_=f_scale.rearrange("o (g p t) -> p (o g) t", p=P, t=PACK))
 
         table_in = keep.tile([P, 1], F32, name="table_in")
         table_out = keep.tile([P, 1], F32, name="table_out")
@@ -62,11 +61,12 @@ def tile_controencodnet_pa_kernel(tc, f_bytes, f_scale, x, w1, b1, out):
         bias_rows = keep.tile([P, P], BF16, name="bias_rows")
         nc.vector.memset(bias_rows[:], 0.0)
 
-        raw = {}
+        raw, raw_two = {}, {}
 
         def load_f(first, count):
             tile = keep.tile([P, count, NODES], U8, name="f_raw%d" % first)
             nc.sync.dma_start(out=tile[:], in_=f_view[:, first : first + count, :])
+            raw_two[first] = tile[:]
             for j in range(count):
                 raw[first + j] = tile[:, j, :]
 
@@ -76,6 +76,7 @@ def tile_controencodnet_pa_kernel(tc, f_bytes, f_scale, x, w1, b1, out):
 
         load_f(0, 1)
         load_f(1, 1)
+        nc.sync.dma_start(out=scale[:], in_=f_scale.rearrange("o (g p t) -> p (o g) t", p=P, t=PACK))
         load_f(2, 2)
         nc.sync.dma_start(out=x_raw[0][:], in_=x_view[0])
         load_f(4, 2)
@@ -101,6 +102,11 @@ def tile_controencodnet_pa_kernel(tc, f_bytes, f_scale, x, w1, b1, out):
             wide[b] = each.tile([P, NODES], BF16, name="wide", align_bytes=64)
             nc.scalar.copy(out=wide[b][:], in_=raw[b].bitcast(FP8))
 
+        def widen_two(b):
+            both = keep.tile([P, 2, NODES], BF16, name="wide_two%d" % b, align_bytes=64)
+            nc.scalar.copy(out=both[:], in_=raw_two[b].bitcast(FP8))
+            wide[b], wide[b + 1] = both[:, 0], both[:, 1]
+
         def turn_pass(dst, b, g):
             words = wide[b][:].bitcast(F32)
             for u in range(2):
@@ -121,12 +127,12 @@ def tile_controencodnet_pa_kernel(tc, f_bytes, f_scale, x, w1, b1, out):
                 op=ALU.mult,
             )
 
-        def first_block():
+        def first_block(borrowed=LAST):
             wide[0] = each.tile([P, NODES], BF16, name="wide", align_bytes=64)
             nc.vector.tensor_copy(out=wide[0][:, :K_PASS], in_=raw[0][:, :K_PASS].bitcast(FP8))
-            nc.scalar.copy(out=wide[0][:, K_PASS:], in_=raw[0][:, K_PASS:].bitcast(FP8))
+            nc.vector.tensor_copy(out=wide[0][:, K_PASS:], in_=raw[0][:, K_PASS:].bitcast(FP8))
             scaled[0] = each.tile([P, PASSES, P, 2, 2], BF16, name="scaled", align_bytes=64)
-            for g, number in enumerate((0, LAST)):
+            for g, number in enumerate((0, borrowed)):
                 half = bank(number)
                 turn_pass(lambda u: half[:, u * P : (u + 1) * P], 0, g)
                 nc.vector.tensor_tensor(
@@ -135,6 +141,27 @@ def tile_controencodnet_pa_kernel(tc, f_bytes, f_scale, x, w1, b1, out):
                     in1=scale[:, g].rearrange("p (u e) -> p u e", e=2).unsqueeze(1).to_broadcast([P, P, 2, 2]),
                     op=ALU.mult,
                 )
+
+        def turn_half(b, g, number):
+            turned[b, g] = bank(number)
+            turn_pass(lambda u: turned[b, g][:, u * P : (u + 1) * P], b, g)
+
+        def scale_half(b, g):
+            if b not in scaled:
+                scaled[b] = each.tile([P, PASSES, P, 2, 2], BF16, name="scaled", align_bytes=64)
+            nc.vector.tensor_tensor(
+                out=scaled[b][:, g],
+                in0=turned[b, g][:, : 2 * P].bitcast(BF16).rearrange("p (u r e) -> p r u e", u=2, e=2),
+                in1=scale[:, g].rearrange("p (u e) -> p u e", e=2).unsqueeze(1).to_broadcast([P, P, 2, 2]),
+                op=ALU.mult,
+            )
+
+        def quantize_half(b, g):
+            if b not in f_mx:
+                f_mx[b] = (each.tile([P, PASSES * P], U32, name="f_codes", align_bytes=64), each.tile([P, PASSES * P], U8, name="f_scales", align_bytes=64))
+            codes, scales = f_mx[b]
+            cols = slice(g * P, (g + 1) * P)
+            nc.vector.quantize_mx(out=codes[:, cols].bitcast(FP8X4), scales=scales[:, cols], in_=scaled[b][:, g].rearrange("p r u e -> p (r u e)"))
 
         def quantize_f(b):
             codes = each.tile([P, PASSES * P], U32, name="f_codes", align_bytes=64)
@@ -158,6 +185,25 @@ def tile_controencodnet_pa_kernel(tc, f_bytes, f_scale, x, w1, b1, out):
             cols = slice(HALF * half, HALF * (half + 1))
             nc.vector.quantize_mx(out=w_codes[:, cols].bitcast(FP8X4), scales=w_scales[:, cols], in_=grouped)
 
+        def group_on_tensor(dst, number, sources):
+            held = bank(number, BF16, 2 * 512)
+            for j, source in enumerate(sources):
+                nc.tensor.matmul(out=held[:, j * 512 : (j + 1) * 512], lhsT=identity_bf[:], rhs=source, start=True, stop=True)
+            return lambda: nc.scalar.copy(out=dst, in_=held[:, : 512 * len(sources)])
+
+        def x_tiles_on_tensor(g, first, count, number):
+            src = x_raw[g][:].rearrange("p t (a s i) -> p s a i t", s=PACK, i=RUN)
+            dst = x_grouped[g][:, first : first + count].rearrange("p s m t -> p (s m t)")
+            return group_on_tensor(dst, number, [src[:, s] for s in range(first, first + count)])
+
+        def group_x_tiles(copy, g, first, end, runs=slice(0, 16)):
+            dst = x_grouped[g][:].rearrange("p s (a i) t -> p a s i t", i=RUN)[:, runs, first:end]
+            copy(dst, x_raw[g][:].rearrange("p t (a s i) -> p a s i t", s=PACK, i=RUN)[:, runs, first:end])
+
+        def w_half_on_tensor(grouped, half, number):
+            src = w_raw[:].rearrange("p t h -> p h t")
+            return group_on_tensor(grouped, number, [src[:, HALF * half + j * P : HALF * half + (j + 1) * P] for j in range(2)])
+
         def first_product(b):
             codes, scales = f_mx[b]
             agg[b] = bank(b)
@@ -175,11 +221,12 @@ def tile_controencodnet_pa_kernel(tc, f_bytes, f_scale, x, w1, b1, out):
                         stop=(g == PASSES - 1),
                     )
 
-        pair_grouped = keep.tile([P, PAIR, P, PACK], BF16, name="pair_grouped", align_bytes=64)
+        where = {b: (n, j) for n, blocks in enumerate(GROUPS) for j, b in enumerate(blocks)}
+        pair_grouped = [keep.tile([P, len(blocks), P, PACK], BF16, name="pair_grouped%d" % n, align_bytes=64) for n, blocks in enumerate(GROUPS)]
 
         def copy_agg(b):
-            if b < PAIR:
-                agg_grouped[b] = pair_grouped[:, b]
+            if b in where:
+                agg_grouped[b] = pair_grouped[where[b][0]][:, where[b][1]]
             else:
                 agg_grouped[b] = each.tile([P, P, PACK], BF16, name="agg_grouped", align_bytes=64)[:]
             nc.scalar.copy(out=agg_grouped[b], in_=agg[b][:].rearrange("p (s r) -> p r s", s=PACK))
@@ -203,6 +250,26 @@ def tile_controencodnet_pa_kernel(tc, f_bytes, f_scale, x, w1, b1, out):
                 stop=True,
             )
 
+        def second_half(b, half, number):
+            codes, scales = agg_mx[b]
+            cols = slice(HALF * half, HALF * (half + 1))
+            second[b, half] = bank(number)
+            nc.tensor.matmul_mx(
+                out=second[b, half][:, cols],
+                lhsT=codes[:].bitcast(FP8X4),
+                lhsT_scale=scales[:],
+                rhs=w_codes[:, cols].bitcast(FP8X4),
+                rhs_scale=w_scales[:, cols],
+                start=True,
+                stop=True,
+            )
+
+        def add_bias_half(b, half):
+            cols = slice(HALF * half, HALF * (half + 1))
+            if b not in biased:
+                biased[b] = each.tile([P, HID], F32, name="biased")
+            nc.vector.tensor_tensor(out=biased[b][:, cols], in0=second[b, half][:, cols], in1=bias[:, cols], op=ALU.add)
+
         def add_bias(b, cols=slice(0, HID)):
             if b not in biased:
                 biased[b] = each.tile([P, HID], F32, name="biased")
@@ -214,123 +281,160 @@ def tile_controencodnet_pa_kernel(tc, f_bytes, f_scale, x, w1, b1, out):
             nc.scalar.activation(out=result[b][:, cols], in_=biased[b][:, cols], func=ACT.Tanh)
             nc.sync.dma_start(out=out_view[:, b, cols], in_=result[b][:, cols])
 
-        pair_tanh = [keep.tile([P, PAIR * P], F32, name="pair_tanh%d" % j, align_bytes=64) for j in range(HID // P)]
+        pair_tanh = [[keep.tile([P, len(blocks) * P], F32, name="pair_tanh%d_%d" % (n, j), align_bytes=64) for j in range(HID // P)] for n, blocks in enumerate(GROUPS)]
+        bias_columns = keep.tile([P, HID // P], F32, name="bias_columns")
+        pair_codes = [keep.tile([P, len(blocks) * P], U32, name="pair_codes%d" % n, align_bytes=64) for n, blocks in enumerate(GROUPS)]
+        pair_scales = [keep.tile([P, len(blocks) * P], U8, name="pair_scales%d" % n, align_bytes=64) for n, blocks in enumerate(GROUPS)]
+        pair_out, empty = {}, {}
 
-        def pair_product(bias_columns):
-            codes = keep.tile([P, PAIR * P], U32, name="pair_codes", align_bytes=64)
-            scales = keep.tile([P, PAIR * P], U8, name="pair_scales", align_bytes=64)
-            nc.vector.quantize_mx(out=codes[:].bitcast(FP8X4), scales=scales[:], in_=pair_grouped[:].rearrange("p b r s -> p (b r s)"))
-            banks = [bank(number) for number in range(PAIR)]
-            tiles = [banks[j // 2][:, (j % 2) * PAIR * P : (j % 2 + 1) * PAIR * P] for j in range(HID // P)]
-            for j, tile in enumerate(tiles):
+        def pair_quantize(n, first, end):
+            cols = slice(first * P, end * P)
+            nc.vector.quantize_mx(out=pair_codes[n][:, cols].bitcast(FP8X4), scales=pair_scales[n][:, cols], in_=pair_grouped[n][:, first:end].rearrange("p b r s -> p (b r s)"))
+
+        def pair_product(n, numbers):
+            width = len(GROUPS[n]) * P
+            banks = [bank(number) for number in numbers]
+            per = HID // P // len(numbers)
+            pair_out[n] = [banks[j // per][:, (j % per) * width : (j % per + 1) * width] for j in range(HID // P)]
+            for j, tile in enumerate(pair_out[n]):
                 cols = slice(j * P, (j + 1) * P)
-                nc.tensor.matmul_mx(
-                    out=tile,
-                    lhsT=w_codes[:, cols].bitcast(FP8X4),
-                    lhsT_scale=w_scales[:, cols],
-                    rhs=codes[:].bitcast(FP8X4),
-                    rhs_scale=scales[:],
-                    start=True,
-                    stop=True,
-                )
-            for j, tile in enumerate(tiles):
-                nc.scalar.activation(out=pair_tanh[j][:], in_=tile, func=ACT.Tanh, bias=bias_columns[:, j : j + 1])
+                for first, end in ([(0, 256), (256, 384)] if width == 384 else [(0, width)]):
+                    nc.tensor.matmul_mx(
+                        out=tile[:, first:end],
+                        lhsT=w_codes[:, cols].bitcast(FP8X4),
+                        lhsT_scale=w_scales[:, cols],
+                        rhs=pair_codes[n][:, first:end].bitcast(FP8X4),
+                        rhs_scale=pair_scales[n][:, first:end],
+                        start=True,
+                        stop=True,
+                    )
+
+        def pair_finish(n):
+            for j, tile in enumerate(pair_out[n]):
+                nc.scalar.activation(out=pair_tanh[n][j][:], in_=tile, func=ACT.Tanh, bias=bias_columns[:, j : j + 1])
 
         def turn_back(b):
             second[b] = bank(b)
+            n, place = where[b]
             for j in range(HID // P):
-                nc.tensor.transpose(second[b][:, j * P : (j + 1) * P], pair_tanh[j][:, b * P : (b + 1) * P], identity[:])
+                nc.tensor.transpose(second[b][:, j * P : (j + 1) * P], pair_tanh[n][j][:, place * P : (place + 1) * P], identity[:])
 
         def store_turned(b):
             result[b] = each.tile([P, HID], F32, name="result")
             nc.scalar.copy(out=result[b][:], in_=second[b][:])
             nc.sync.dma_start(out=out_view[:, b, :], in_=result[b][:])
 
+        def store_turned_vector(b):
+            result[b] = each.tile([P, HID], F32, name="result")
+            nc.vector.tensor_copy(out=result[b][:], in_=second[b][:])
+            nc.sync.dma_start(out=out_view[:, b, :], in_=result[b][:])
+
         def scalar_copy(dst, src):
             nc.scalar.copy(out=dst, in_=src)
 
-        first_block()
-        for b in range(1, 4):
-            widen(b)
-            turn(b)
-            scale_out(b)
-        group_x(gpsimd_copy, 0, 0, X_COLS_ON_GPSIMD)
-        group_x(scalar_copy, 0, X_COLS_ON_GPSIMD, FEATS)
-        for b in (4, 5):
-            widen(b)
-            turn(b)
-        group_x(scalar_copy, 1, 0, FEATS)
+        def vector_copy(dst, src):
+            nc.vector.tensor_copy(out=dst, in_=src)
 
+        x1_flat = x_grouped[1][:].rearrange("p s m t -> p (s m t)")
+        w_grouped = [keep.tile([P, PACK * HALF], BF16, name="w_grouped", align_bytes=64)[:], x1_flat[:, : PACK * HALF]]
+
+        first_block(7)
+        widen(1)
+        turn(1)
+        scale_out(1)
+        widen(2)
+        turn(2)
+        scale_out(2)
+        widen(3)
+        turn(3)
+        scale_out(3)
+        group_x_tiles(gpsimd_copy, 0, 0, 4, slice(0, 12))
+        group_x_tiles(scalar_copy, 0, 0, 4, slice(12, 16))
+        widen(4)
+        warm = bank(6)
+        for unused in range(1):
+            nc.tensor.matmul(out=warm[:, :P], lhsT=identity[:], rhs=identity[:], start=True, stop=True)
+        widen(5)
+        group_x_tiles(scalar_copy, 1, 2, 4)
+        empty["X10"] = x_tiles_on_tensor(1, 0, 2, 0)
+        empty["X10"]()
+        turn(4)
+        turn(5)
         bias_turned = bank(2, BF16, 2 * 512)
         nc.tensor.transpose(bias_turned[:, :P], bias_rows[:], identity_bf[:])
-
-        warm = bank(1)
-        for unused in range(4):
-            nc.tensor.matmul(out=warm[:], lhsT=identity_bf[:], rhs=wide[1][:, :512], start=True, stop=True)
-
         widen(6)
-        bias_columns = keep.tile([P, HID // P], F32, name="bias_columns")
-        nc.scalar.copy(out=bias_columns[:], in_=bias_turned[:, : HID // P])
+        empty["W0"] = w_half_on_tensor(w_grouped[0], 0, 1)
+        widen(7)
+        empty["W0"]()
         turn(6)
-
+        nc.scalar.copy(out=bias_columns[:], in_=bias_turned[:, : HID // P])
         quantize_x(0)
-        for b in range(3):
-            quantize_f(b)
+        quantize_f(0)
+        quantize_f(1)
         quantize_x(1)
+        quantize_f(2)
         quantize_f(3)
-
-        w_grouped = [keep.tile([P, PACK * HALF], BF16, name="w_grouped", align_bytes=64)[:], scaled[3][:].rearrange("p g r u e -> p (g r u e)")]
-        group_w(scalar_copy, w_grouped[0], 0, 0, HALF)
-        widen(LAST)
-        group_w(gpsimd_copy, w_grouped[1], 1, 0, W_COLS_ON_GPSIMD)
-        group_w(scalar_copy, w_grouped[1], 1, W_COLS_ON_GPSIMD, HALF)
+        w_grouped[1] = scaled[3][:].rearrange("p g r u e -> p (g r u e)")
+        group_w(gpsimd_copy, w_grouped[1], 1, 0, 192)
+        group_w(scalar_copy, w_grouped[1], 1, 192, 256)
         scale_out(4)
         scale_out(5)
+        first_product(0)
+        copy_agg(0)
+        first_product(1)
+        copy_agg(1)
+        first_product(2)
+        copy_agg(2)
+        first_product(3)
+        copy_agg(3)
         quantize_f(4)
-        for b in range(5):
-            first_product(b)
-            copy_agg(b)
-        for half in range(2):
-            quantize_w(w_grouped[half], half)
-        pair_product(bias_columns)
-
-        quantize_f(5)
+        quantize_w(w_grouped[0], 0)
+        pair_quantize(0, 0, 2)
+        quantize_w(w_grouped[1], 1)
+        first_product(4)
+        copy_agg(4)
+        pair_product(0, (0, 1,))
+        pair_finish(0)
         quantize_agg(2)
+        quantize_f(5)
         second_product(2)
         first_product(5)
-        turn(LAST)
+        turn(7)
         scale_out(6)
-        quantize_agg(3)
         add_bias(2)
-        quantize_agg(4)
+        quantize_agg(3)
         quantize_f(6)
         copy_agg(5)
         finish(2)
-        for b in range(PAIR):
-            turn_back(b)
+        turn_back(0)
+        turn_back(1)
         store_turned(0)
         first_product(6)
         copy_agg(6)
         store_turned(1)
-        scale_out(LAST)
+        scale_out(7)
+        quantize_agg(4)
         quantize_agg(5)
-        quantize_f(LAST)
-
-        for b in range(3, 6):
-            second_product(b)
-        first_product(LAST)
+        quantize_f(7)
+        second_product(3)
+        second_product(4)
+        second_product(5)
+        first_product(7)
         add_bias(3)
         finish(3)
         quantize_agg(6)
         second_product(6)
-        copy_agg(LAST)
-        for b in range(4, LAST):
-            add_bias(b)
-            finish(b)
-
-        quantize_agg(LAST)
-        second_product(LAST)
-        for half in range(2):
-            cols = slice(HALF * half, HALF * (half + 1))
-            add_bias(LAST, cols)
-            finish(LAST, cols)
+        copy_agg(7)
+        add_bias(4)
+        finish(4)
+        add_bias(5)
+        finish(5)
+        add_bias(6)
+        finish(6)
+        quantize_agg(7)
+        second_half(7, 0, 7)
+        second_half(7, 1, 0)
+        add_bias_half(7, 0)
+        finish(7, slice(0, SPLIT))
+        add_bias_half(7, 1)
+        finish(7, slice(SPLIT, HID))

@@ -25,8 +25,8 @@ PAIR = 2
 HALF = HID // 2
 LAST = BLOCKS - 1
 
-GROUPS = [(0, 1)]
-SPLIT = 256
+X_TILES_ON_GPSIMD = 3
+W_COLS_ON_GPSIMD = 192
 
 
 def tile_controencodnet_pa_kernel(tc, f_bytes, f_scale, x, w1, b1, out):
@@ -48,7 +48,8 @@ def tile_controencodnet_pa_kernel(tc, f_bytes, f_scale, x, w1, b1, out):
         def gpsimd_copy(dst, src):
             nc.gpsimd.tensor_scalar(out=dst, in0=src, scalar1=1.0, scalar2=0.0, op0=ALU.mult, op1=ALU.add)
 
-        scale = keep.tile([P, PASSES, PACK], F32, name="scale")
+        zeros = keep.tile([P, 2 * P], F32, name="zeros")
+        nc.vector.memset(zeros[:], 0.0)
 
         table_in = keep.tile([P, 1], F32, name="table_in")
         table_out = keep.tile([P, 1], F32, name="table_out")
@@ -61,12 +62,11 @@ def tile_controencodnet_pa_kernel(tc, f_bytes, f_scale, x, w1, b1, out):
         bias_rows = keep.tile([P, P], BF16, name="bias_rows")
         nc.vector.memset(bias_rows[:], 0.0)
 
-        raw, raw_two = {}, {}
+        raw = {}
 
         def load_f(first, count):
             tile = keep.tile([P, count, NODES], U8, name="f_raw%d" % first)
             nc.sync.dma_start(out=tile[:], in_=f_view[:, first : first + count, :])
-            raw_two[first] = tile[:]
             for j in range(count):
                 raw[first + j] = tile[:, j, :]
 
@@ -76,6 +76,7 @@ def tile_controencodnet_pa_kernel(tc, f_bytes, f_scale, x, w1, b1, out):
 
         load_f(0, 1)
         load_f(1, 1)
+        scale = keep.tile([P, PASSES, PACK], F32, name="scale")
         nc.sync.dma_start(out=scale[:], in_=f_scale.rearrange("o (g p t) -> p (o g) t", p=P, t=PACK))
         load_f(2, 2)
         nc.sync.dma_start(out=x_raw[0][:], in_=x_view[0])
@@ -96,16 +97,14 @@ def tile_controencodnet_pa_kernel(tc, f_bytes, f_scale, x, w1, b1, out):
         w_codes = keep.tile([P, HID], U32, name="w_codes", align_bytes=64)
         w_scales = keep.tile([P, HID], U8, name="w_scales", align_bytes=64)
 
+        scaled_pair = [keep.tile([P, 2 * NODES], BF16, name="scaled_pair%d" % n, align_bytes=64) for n in range(2)]
+        w_grouped = [keep.tile([P, PACK * HALF], BF16, name="w_grouped", align_bytes=64)[:], scaled_pair[1][:, NODES:]]
+
         wide, turned, scaled, f_mx, agg, agg_grouped, agg_mx, second, biased, result = ({} for unused in range(10))
 
         def widen(b):
             wide[b] = each.tile([P, NODES], BF16, name="wide", align_bytes=64)
             nc.scalar.copy(out=wide[b][:], in_=raw[b].bitcast(FP8))
-
-        def widen_two(b):
-            both = keep.tile([P, 2, NODES], BF16, name="wide_two%d" % b, align_bytes=64)
-            nc.scalar.copy(out=both[:], in_=raw_two[b].bitcast(FP8))
-            wide[b], wide[b + 1] = both[:, 0], both[:, 1]
 
         def turn_pass(dst, b, g):
             words = wide[b][:].bitcast(F32)
@@ -118,91 +117,74 @@ def tile_controencodnet_pa_kernel(tc, f_bytes, f_scale, x, w1, b1, out):
             for g in range(PASSES):
                 turn_pass(lambda u: view[:, u, g, :], b, g)
 
+        def scaled_tile(b):
+            if b < 4:
+                return scaled_pair[b // 2][:, (b % 2) * NODES : (b % 2 + 1) * NODES]
+            return each.tile([P, NODES], BF16, name="scaled", align_bytes=64)[:]
+
         def scale_out(b):
-            scaled[b] = each.tile([P, PASSES, P, 2, 2], BF16, name="scaled", align_bytes=64)
+            scaled[b] = scaled_tile(b)
             nc.vector.tensor_tensor(
-                out=scaled[b][:],
+                out=scaled[b].rearrange("p (g r u e) -> p g r u e", g=PASSES, u=2, e=2),
                 in0=turned[b][:].bitcast(BF16).rearrange("p (u g r e) -> p g r u e", u=2, g=PASSES, e=2),
                 in1=scale[:].rearrange("p g (u e) -> p g u e", e=2).unsqueeze(2).to_broadcast([P, PASSES, P, 2, 2]),
                 op=ALU.mult,
             )
 
-        def first_block(borrowed=LAST):
+        def first_block():
             wide[0] = each.tile([P, NODES], BF16, name="wide", align_bytes=64)
-            nc.vector.tensor_copy(out=wide[0][:, :K_PASS], in_=raw[0][:, :K_PASS].bitcast(FP8))
-            nc.vector.tensor_copy(out=wide[0][:, K_PASS:], in_=raw[0][:, K_PASS:].bitcast(FP8))
-            scaled[0] = each.tile([P, PASSES, P, 2, 2], BF16, name="scaled", align_bytes=64)
-            for g, number in enumerate((0, borrowed)):
+            for g in range(PASSES):
+                cols = slice(g * K_PASS, (g + 1) * K_PASS)
+                nc.vector.tensor_copy(out=wide[0][:, cols], in_=raw[0][:, cols].bitcast(FP8))
+            scaled[0] = scaled_tile(0)
+            for g, number in enumerate((0, LAST)):
                 half = bank(number)
                 turn_pass(lambda u: half[:, u * P : (u + 1) * P], 0, g)
                 nc.vector.tensor_tensor(
-                    out=scaled[0][:, g],
+                    out=scaled[0].rearrange("p (g r u e) -> p g r u e", g=PASSES, u=2, e=2)[:, g],
                     in0=half[:, : 2 * P].bitcast(BF16).rearrange("p (u r e) -> p r u e", u=2, e=2),
                     in1=scale[:, g].rearrange("p (u e) -> p u e", e=2).unsqueeze(1).to_broadcast([P, P, 2, 2]),
                     op=ALU.mult,
                 )
 
-        def turn_half(b, g, number):
-            turned[b, g] = bank(number)
-            turn_pass(lambda u: turned[b, g][:, u * P : (u + 1) * P], b, g)
-
-        def scale_half(b, g):
-            if b not in scaled:
-                scaled[b] = each.tile([P, PASSES, P, 2, 2], BF16, name="scaled", align_bytes=64)
-            nc.vector.tensor_tensor(
-                out=scaled[b][:, g],
-                in0=turned[b, g][:, : 2 * P].bitcast(BF16).rearrange("p (u r e) -> p r u e", u=2, e=2),
-                in1=scale[:, g].rearrange("p (u e) -> p u e", e=2).unsqueeze(1).to_broadcast([P, P, 2, 2]),
-                op=ALU.mult,
-            )
-
-        def quantize_half(b, g):
-            if b not in f_mx:
-                f_mx[b] = (each.tile([P, PASSES * P], U32, name="f_codes", align_bytes=64), each.tile([P, PASSES * P], U8, name="f_scales", align_bytes=64))
-            codes, scales = f_mx[b]
-            cols = slice(g * P, (g + 1) * P)
-            nc.vector.quantize_mx(out=codes[:, cols].bitcast(FP8X4), scales=scales[:, cols], in_=scaled[b][:, g].rearrange("p r u e -> p (r u e)"))
-
-        def quantize_f(b):
-            codes = each.tile([P, PASSES * P], U32, name="f_codes", align_bytes=64)
-            scales = each.tile([P, PASSES * P], U8, name="f_scales", align_bytes=64)
-            nc.vector.quantize_mx(out=codes[:].bitcast(FP8X4), scales=scales[:], in_=scaled[b][:].rearrange("p g r u e -> p (g r u e)"))
-            f_mx[b] = (codes, scales)
+        def quantize_f(first, count=1):
+            width = PASSES * P
+            codes = keep.tile([P, count * width], U32, name="f_codes%d" % first, align_bytes=64)
+            scales = keep.tile([P, count * width], U8, name="f_scales%d" % first, align_bytes=64)
+            source = scaled[first] if count == 1 else scaled_pair[first // 2][:]
+            nc.vector.quantize_mx(out=codes[:].bitcast(FP8X4), scales=scales[:], in_=source)
+            for j in range(count):
+                f_mx[first + j] = (codes[:, j * width : (j + 1) * width], scales[:, j * width : (j + 1) * width])
 
         def group_x(copy, g, first, end):
-            runs = slice(first // (PACK * RUN), end // (PACK * RUN))
-            dst = x_grouped[g][:].rearrange("p s (a i) t -> p a s i t", i=RUN)[:, runs]
-            copy(dst, x_raw[g][:].rearrange("p t (a s i) -> p a s i t", s=PACK, i=RUN)[:, runs])
+            dst = x_grouped[g][:].rearrange("p s (a i) t -> p a s i t", i=RUN)[:, :, first:end]
+            copy(dst, x_raw[g][:].rearrange("p t (a s i) -> p a s i t", s=PACK, i=RUN)[:, :, first:end])
+
+        def group_on_tensor(sources, number):
+            held = bank(number, BF16, 2 * 512)
+            for j, source in enumerate(sources):
+                nc.tensor.matmul(out=held[:, j * 512 : (j + 1) * 512], lhsT=identity_bf[:], rhs=source, start=True, stop=True)
+            return held[:, : len(sources) * 512]
+
+        def group_x_on_tensor(g, first, end, number):
+            tiles = x_raw[g][:].rearrange("p t (a s i) -> p s a i t", s=PACK, i=RUN)
+            return group_on_tensor([tiles[:, s] for s in range(first, end)], number)
+
+        def x_tiles(g, first, end):
+            return x_grouped[g][:, first:end].rearrange("p s m t -> p (s m t)")
 
         def quantize_x(g):
             nc.vector.quantize_mx(out=x_codes[g][:].bitcast(FP8X4), scales=x_scales[g][:], in_=x_grouped[g][:].rearrange("p s m t -> p (s m t)"))
 
-        def group_w(copy, grouped, half, first, end):
-            src = w_raw[:, :, HALF * half + first : HALF * half + end].rearrange("p t h -> p h t")
-            copy(grouped.rearrange("p (h t) -> p h t", t=PACK)[:, first:end], src)
+        w_columns = w_raw[:].rearrange("p t h -> p h t")
 
-        def quantize_w(grouped, half):
+        def group_w(copy, half, first, end):
+            src = w_columns[:, HALF * half + first : HALF * half + end]
+            copy(w_grouped[half].rearrange("p (h t) -> p h t", t=PACK)[:, first:end], src)
+
+        def quantize_w(half):
             cols = slice(HALF * half, HALF * (half + 1))
-            nc.vector.quantize_mx(out=w_codes[:, cols].bitcast(FP8X4), scales=w_scales[:, cols], in_=grouped)
-
-        def group_on_tensor(dst, number, sources):
-            held = bank(number, BF16, 2 * 512)
-            for j, source in enumerate(sources):
-                nc.tensor.matmul(out=held[:, j * 512 : (j + 1) * 512], lhsT=identity_bf[:], rhs=source, start=True, stop=True)
-            return lambda: nc.scalar.copy(out=dst, in_=held[:, : 512 * len(sources)])
-
-        def x_tiles_on_tensor(g, first, count, number):
-            src = x_raw[g][:].rearrange("p t (a s i) -> p s a i t", s=PACK, i=RUN)
-            dst = x_grouped[g][:, first : first + count].rearrange("p s m t -> p (s m t)")
-            return group_on_tensor(dst, number, [src[:, s] for s in range(first, first + count)])
-
-        def group_x_tiles(copy, g, first, end, runs=slice(0, 16)):
-            dst = x_grouped[g][:].rearrange("p s (a i) t -> p a s i t", i=RUN)[:, runs, first:end]
-            copy(dst, x_raw[g][:].rearrange("p t (a s i) -> p a s i t", s=PACK, i=RUN)[:, runs, first:end])
-
-        def w_half_on_tensor(grouped, half, number):
-            src = w_raw[:].rearrange("p t h -> p h t")
-            return group_on_tensor(grouped, number, [src[:, HALF * half + j * P : HALF * half + (j + 1) * P] for j in range(2)])
+            nc.vector.quantize_mx(out=w_codes[:, cols].bitcast(FP8X4), scales=w_scales[:, cols], in_=w_grouped[half])
 
         def first_product(b):
             codes, scales = f_mx[b]
@@ -221,12 +203,11 @@ def tile_controencodnet_pa_kernel(tc, f_bytes, f_scale, x, w1, b1, out):
                         stop=(g == PASSES - 1),
                     )
 
-        where = {b: (n, j) for n, blocks in enumerate(GROUPS) for j, b in enumerate(blocks)}
-        pair_grouped = [keep.tile([P, len(blocks), P, PACK], BF16, name="pair_grouped%d" % n, align_bytes=64) for n, blocks in enumerate(GROUPS)]
+        pair_grouped = keep.tile([P, PAIR, P, PACK], BF16, name="pair_grouped", align_bytes=64)
 
         def copy_agg(b):
-            if b in where:
-                agg_grouped[b] = pair_grouped[where[b][0]][:, where[b][1]]
+            if b < PAIR:
+                agg_grouped[b] = pair_grouped[:, b]
             else:
                 agg_grouped[b] = each.tile([P, P, PACK], BF16, name="agg_grouped", align_bytes=64)[:]
             nc.scalar.copy(out=agg_grouped[b], in_=agg[b][:].rearrange("p (s r) -> p r s", s=PACK))
@@ -237,25 +218,11 @@ def tile_controencodnet_pa_kernel(tc, f_bytes, f_scale, x, w1, b1, out):
             nc.vector.quantize_mx(out=codes[:].bitcast(FP8X4), scales=scales[:], in_=agg_grouped[b].rearrange("p r s -> p (r s)"))
             agg_mx[b] = (codes, scales)
 
-        def second_product(b):
+        def second_product(b, cols=slice(0, HID), number=None):
             codes, scales = agg_mx[b]
-            second[b] = bank(b)
+            second[b, cols.start] = bank(b if number is None else number)[:, cols]
             nc.tensor.matmul_mx(
-                out=second[b][:],
-                lhsT=codes[:].bitcast(FP8X4),
-                lhsT_scale=scales[:],
-                rhs=w_codes[:].bitcast(FP8X4),
-                rhs_scale=w_scales[:],
-                start=True,
-                stop=True,
-            )
-
-        def second_half(b, half, number):
-            codes, scales = agg_mx[b]
-            cols = slice(HALF * half, HALF * (half + 1))
-            second[b, half] = bank(number)
-            nc.tensor.matmul_mx(
-                out=second[b, half][:, cols],
+                out=second[b, cols.start],
                 lhsT=codes[:].bitcast(FP8X4),
                 lhsT_scale=scales[:],
                 rhs=w_codes[:, cols].bitcast(FP8X4),
@@ -264,16 +231,10 @@ def tile_controencodnet_pa_kernel(tc, f_bytes, f_scale, x, w1, b1, out):
                 stop=True,
             )
 
-        def add_bias_half(b, half):
-            cols = slice(HALF * half, HALF * (half + 1))
-            if b not in biased:
-                biased[b] = each.tile([P, HID], F32, name="biased")
-            nc.vector.tensor_tensor(out=biased[b][:, cols], in0=second[b, half][:, cols], in1=bias[:, cols], op=ALU.add)
-
         def add_bias(b, cols=slice(0, HID)):
             if b not in biased:
                 biased[b] = each.tile([P, HID], F32, name="biased")
-            nc.vector.tensor_tensor(out=biased[b][:, cols], in0=second[b][:, cols], in1=bias[:, cols], op=ALU.add)
+            nc.vector.tensor_tensor(out=biased[b][:, cols], in0=second[b, cols.start], in1=bias[:, cols], op=ALU.add)
 
         def finish(b, cols=slice(0, HID)):
             if b not in result:
@@ -281,160 +242,131 @@ def tile_controencodnet_pa_kernel(tc, f_bytes, f_scale, x, w1, b1, out):
             nc.scalar.activation(out=result[b][:, cols], in_=biased[b][:, cols], func=ACT.Tanh)
             nc.sync.dma_start(out=out_view[:, b, cols], in_=result[b][:, cols])
 
-        pair_tanh = [[keep.tile([P, len(blocks) * P], F32, name="pair_tanh%d_%d" % (n, j), align_bytes=64) for j in range(HID // P)] for n, blocks in enumerate(GROUPS)]
-        bias_columns = keep.tile([P, HID // P], F32, name="bias_columns")
-        pair_codes = [keep.tile([P, len(blocks) * P], U32, name="pair_codes%d" % n, align_bytes=64) for n, blocks in enumerate(GROUPS)]
-        pair_scales = [keep.tile([P, len(blocks) * P], U8, name="pair_scales%d" % n, align_bytes=64) for n, blocks in enumerate(GROUPS)]
-        pair_out, empty = {}, {}
+        pair_tanh = [keep.tile([P, PAIR * P], F32, name="pair_tanh%d" % j, align_bytes=64) for j in range(HID // P)]
 
-        def pair_quantize(n, first, end):
-            cols = slice(first * P, end * P)
-            nc.vector.quantize_mx(out=pair_codes[n][:, cols].bitcast(FP8X4), scales=pair_scales[n][:, cols], in_=pair_grouped[n][:, first:end].rearrange("p b r s -> p (b r s)"))
-
-        def pair_product(n, numbers):
-            width = len(GROUPS[n]) * P
-            banks = [bank(number) for number in numbers]
-            per = HID // P // len(numbers)
-            pair_out[n] = [banks[j // per][:, (j % per) * width : (j % per + 1) * width] for j in range(HID // P)]
-            for j, tile in enumerate(pair_out[n]):
+        def pair_product(bias_columns):
+            codes = keep.tile([P, PAIR * P], U32, name="pair_codes", align_bytes=64)
+            scales = keep.tile([P, PAIR * P], U8, name="pair_scales", align_bytes=64)
+            nc.vector.quantize_mx(out=codes[:].bitcast(FP8X4), scales=scales[:], in_=pair_grouped[:].rearrange("p b r s -> p (b r s)"))
+            quantize_w(1)
+            banks = [bank(number) for number in range(PAIR)]
+            tiles = [banks[j // 2][:, (j % 2) * PAIR * P : (j % 2 + 1) * PAIR * P] for j in range(HID // P)]
+            for j, tile in enumerate(tiles):
                 cols = slice(j * P, (j + 1) * P)
-                for first, end in ([(0, 256), (256, 384)] if width == 384 else [(0, width)]):
-                    nc.tensor.matmul_mx(
-                        out=tile[:, first:end],
-                        lhsT=w_codes[:, cols].bitcast(FP8X4),
-                        lhsT_scale=w_scales[:, cols],
-                        rhs=pair_codes[n][:, first:end].bitcast(FP8X4),
-                        rhs_scale=pair_scales[n][:, first:end],
-                        start=True,
-                        stop=True,
-                    )
-
-        def pair_finish(n):
-            for j, tile in enumerate(pair_out[n]):
-                nc.scalar.activation(out=pair_tanh[n][j][:], in_=tile, func=ACT.Tanh, bias=bias_columns[:, j : j + 1])
+                nc.tensor.matmul_mx(
+                    out=tile,
+                    lhsT=w_codes[:, cols].bitcast(FP8X4),
+                    lhsT_scale=w_scales[:, cols],
+                    rhs=codes[:].bitcast(FP8X4),
+                    rhs_scale=scales[:],
+                    start=True,
+                    stop=True,
+                )
+            for j, tile in enumerate(tiles):
+                nc.scalar.activation(out=pair_tanh[j][:], in_=tile, func=ACT.Tanh, bias=bias_columns[:, j : j + 1])
 
         def turn_back(b):
             second[b] = bank(b)
-            n, place = where[b]
             for j in range(HID // P):
-                nc.tensor.transpose(second[b][:, j * P : (j + 1) * P], pair_tanh[n][j][:, place * P : (place + 1) * P], identity[:])
+                nc.tensor.transpose(second[b][:, j * P : (j + 1) * P], pair_tanh[j][:, b * P : (b + 1) * P], identity[:])
 
         def store_turned(b):
             result[b] = each.tile([P, HID], F32, name="result")
             nc.scalar.copy(out=result[b][:], in_=second[b][:])
             nc.sync.dma_start(out=out_view[:, b, :], in_=result[b][:])
 
-        def store_turned_vector(b):
-            result[b] = each.tile([P, HID], F32, name="result")
-            nc.vector.tensor_copy(out=result[b][:], in_=second[b][:])
-            nc.sync.dma_start(out=out_view[:, b, :], in_=result[b][:])
-
         def scalar_copy(dst, src):
             nc.scalar.copy(out=dst, in_=src)
 
-        def vector_copy(dst, src):
-            nc.vector.tensor_copy(out=dst, in_=src)
+        def warm_up(width, target):
+            nc.tensor.matmul(out=target[:, :width], lhsT=zeros[:, :P], rhs=zeros[:, :width], start=True, stop=True)
 
-        x1_flat = x_grouped[1][:].rearrange("p s m t -> p (s m t)")
-        w_grouped = [keep.tile([P, PACK * HALF], BF16, name="w_grouped", align_bytes=64)[:], x1_flat[:, : PACK * HALF]]
-
-        first_block(7)
-        widen(1)
-        turn(1)
-        scale_out(1)
-        widen(2)
-        turn(2)
-        scale_out(2)
-        widen(3)
-        turn(3)
-        scale_out(3)
-        group_x_tiles(gpsimd_copy, 0, 0, 4, slice(0, 12))
-        group_x_tiles(scalar_copy, 0, 0, 4, slice(12, 16))
-        widen(4)
         warm = bank(6)
-        for unused in range(1):
-            nc.tensor.matmul(out=warm[:, :P], lhsT=identity[:], rhs=identity[:], start=True, stop=True)
+        for unused in range(2):
+            warm_up(224, warm)
+        first_block()
+        for b in range(1, 4):
+            widen(b)
+            turn(b)
+            if b != 2:
+                warm_up(256, warm)
+            scale_out(b)
+        group_x(gpsimd_copy, 0, 0, X_TILES_ON_GPSIMD)
+        group_x(scalar_copy, 0, X_TILES_ON_GPSIMD, PACK)
+        widen(4)
         widen(5)
-        group_x_tiles(scalar_copy, 1, 2, 4)
-        empty["X10"] = x_tiles_on_tensor(1, 0, 2, 0)
-        empty["X10"]()
+
+        group_x(scalar_copy, 1, 2, PACK)
+        scalar_copy(x_tiles(1, 0, 2), group_x_on_tensor(1, 0, 2, 0))
         turn(4)
         turn(5)
+
         bias_turned = bank(2, BF16, 2 * 512)
         nc.tensor.transpose(bias_turned[:, :P], bias_rows[:], identity_bf[:])
+        warm_up(256, warm)
+
         widen(6)
-        empty["W0"] = w_half_on_tensor(w_grouped[0], 0, 1)
-        widen(7)
-        empty["W0"]()
+        group_w(scalar_copy, 0, 0, HALF)
         turn(6)
+        widen(LAST)
+        bias_columns = keep.tile([P, HID // P], F32, name="bias_columns")
         nc.scalar.copy(out=bias_columns[:], in_=bias_turned[:, : HID // P])
+
         quantize_x(0)
-        quantize_f(0)
-        quantize_f(1)
+        quantize_f(0, 2)
         quantize_x(1)
-        quantize_f(2)
-        quantize_f(3)
-        w_grouped[1] = scaled[3][:].rearrange("p g r u e -> p (g r u e)")
-        group_w(gpsimd_copy, w_grouped[1], 1, 0, 192)
-        group_w(scalar_copy, w_grouped[1], 1, 192, 256)
+        quantize_f(2, 2)
+
+        group_w(gpsimd_copy, 1, 0, W_COLS_ON_GPSIMD)
+        group_w(scalar_copy, 1, W_COLS_ON_GPSIMD, HALF)
         scale_out(4)
         scale_out(5)
-        first_product(0)
-        copy_agg(0)
-        first_product(1)
-        copy_agg(1)
-        first_product(2)
-        copy_agg(2)
-        first_product(3)
-        copy_agg(3)
         quantize_f(4)
-        quantize_w(w_grouped[0], 0)
-        pair_quantize(0, 0, 2)
-        quantize_w(w_grouped[1], 1)
-        first_product(4)
-        copy_agg(4)
-        pair_product(0, (0, 1,))
-        pair_finish(0)
+        for b in range(5):
+            first_product(b)
+            copy_agg(b)
+        quantize_w(0)
+        pair_product(bias_columns)
+
         quantize_agg(2)
         quantize_f(5)
         second_product(2)
         first_product(5)
-        turn(7)
+        turn(LAST)
         scale_out(6)
         add_bias(2)
         quantize_agg(3)
         quantize_f(6)
         copy_agg(5)
         finish(2)
-        turn_back(0)
-        turn_back(1)
+        for b in range(PAIR):
+            turn_back(b)
         store_turned(0)
         first_product(6)
         copy_agg(6)
         store_turned(1)
-        scale_out(7)
+        scale_out(LAST)
         quantize_agg(4)
         quantize_agg(5)
-        quantize_f(7)
-        second_product(3)
-        second_product(4)
-        second_product(5)
-        first_product(7)
+        quantize_f(LAST)
+
+        for b in range(3, 6):
+            second_product(b)
+        first_product(LAST)
         add_bias(3)
         finish(3)
         quantize_agg(6)
         second_product(6)
-        copy_agg(7)
-        add_bias(4)
-        finish(4)
-        add_bias(5)
-        finish(5)
-        add_bias(6)
-        finish(6)
-        quantize_agg(7)
-        second_half(7, 0, 7)
-        second_half(7, 1, 0)
-        add_bias_half(7, 0)
-        finish(7, slice(0, SPLIT))
-        add_bias_half(7, 1)
-        finish(7, slice(SPLIT, HID))
+        warm_up(128, bank(1))
+        copy_agg(LAST)
+        for b in range(4, LAST):
+            add_bias(b)
+            finish(b)
+
+        quantize_agg(LAST)
+        halves = [slice(HALF * half, HALF * (half + 1)) for half in range(2)]
+        for cols, number in zip(halves, (LAST, 0)):
+            second_product(LAST, cols, number)
+        for cols in halves:
+            add_bias(LAST, cols)
+            finish(LAST, cols)

@@ -23,10 +23,16 @@ K_PASS = P * PACK
 RUN = 8
 PAIR = 2
 HALF = HID // 2
+BANK = 512
 LAST = BLOCKS - 1
 
 X_TILES_ON_GPSIMD = 3
 W_COLS_ON_GPSIMD = 192
+X_TILES_ON_TENSOR = 2
+
+WARM_FIRST = 224
+WARM_BETWEEN = 256
+WARM_LAST = 128
 
 
 def tile_controencodnet_pa_kernel(tc, f_bytes, f_scale, x, w1, b1, out):
@@ -42,13 +48,13 @@ def tile_controencodnet_pa_kernel(tc, f_bytes, f_scale, x, w1, b1, out):
         psum = ctx.enter_context(tc.psum_pool(name="psum", bufs=1))
         ctx.enter_context(tc.manual_schedule())
 
-        def bank(number, dtype=F32, columns=512):
+        def bank(number, dtype=F32, columns=BANK):
             return psum.tile([P, columns], dtype, name="bank%d" % number)
 
         def gpsimd_copy(dst, src):
             nc.gpsimd.tensor_scalar(out=dst, in0=src, scalar1=1.0, scalar2=0.0, op0=ALU.mult, op1=ALU.add)
 
-        zeros = keep.tile([P, 2 * P], F32, name="zeros")
+        zeros = keep.tile([P, WARM_BETWEEN], F32, name="zeros")
         nc.vector.memset(zeros[:], 0.0)
 
         table_in = keep.tile([P, 1], F32, name="table_in")
@@ -100,7 +106,7 @@ def tile_controencodnet_pa_kernel(tc, f_bytes, f_scale, x, w1, b1, out):
         scaled_pair = [keep.tile([P, 2 * NODES], BF16, name="scaled_pair%d" % n, align_bytes=64) for n in range(2)]
         w_grouped = [keep.tile([P, PACK * HALF], BF16, name="w_grouped", align_bytes=64)[:], scaled_pair[1][:, NODES:]]
 
-        wide, turned, scaled, f_mx, agg, agg_grouped, agg_mx, second, biased, result = ({} for unused in range(10))
+        wide, turned, scaled, f_mx, agg, agg_grouped, agg_mx, second, back, biased, result = ({} for unused in range(11))
 
         def widen(b):
             wide[b] = each.tile([P, NODES], BF16, name="wide", align_bytes=64)
@@ -118,7 +124,7 @@ def tile_controencodnet_pa_kernel(tc, f_bytes, f_scale, x, w1, b1, out):
                 turn_pass(lambda u: view[:, u, g, :], b, g)
 
         def scaled_tile(b):
-            if b < 4:
+            if b < 2 * len(scaled_pair):
                 return scaled_pair[b // 2][:, (b % 2) * NODES : (b % 2 + 1) * NODES]
             return each.tile([P, NODES], BF16, name="scaled", align_bytes=64)[:]
 
@@ -160,26 +166,18 @@ def tile_controencodnet_pa_kernel(tc, f_bytes, f_scale, x, w1, b1, out):
             dst = x_grouped[g][:].rearrange("p s (a i) t -> p a s i t", i=RUN)[:, :, first:end]
             copy(dst, x_raw[g][:].rearrange("p t (a s i) -> p a s i t", s=PACK, i=RUN)[:, :, first:end])
 
-        def group_on_tensor(sources, number):
-            held = bank(number, BF16, 2 * 512)
-            for j, source in enumerate(sources):
-                nc.tensor.matmul(out=held[:, j * 512 : (j + 1) * 512], lhsT=identity_bf[:], rhs=source, start=True, stop=True)
-            return held[:, : len(sources) * 512]
-
-        def group_x_on_tensor(g, first, end, number):
+        def group_x_on_tensor(g, count, number):
             tiles = x_raw[g][:].rearrange("p t (a s i) -> p s a i t", s=PACK, i=RUN)
-            return group_on_tensor([tiles[:, s] for s in range(first, end)], number)
-
-        def x_tiles(g, first, end):
-            return x_grouped[g][:, first:end].rearrange("p s m t -> p (s m t)")
+            held = bank(number, BF16, 2 * BANK)
+            for s in range(count):
+                nc.tensor.matmul(out=held[:, s * BANK : (s + 1) * BANK], lhsT=identity_bf[:], rhs=tiles[:, s], start=True, stop=True)
+            nc.scalar.copy(out=x_grouped[g][:, :count].rearrange("p s m t -> p (s m t)"), in_=held[:, : count * BANK])
 
         def quantize_x(g):
             nc.vector.quantize_mx(out=x_codes[g][:].bitcast(FP8X4), scales=x_scales[g][:], in_=x_grouped[g][:].rearrange("p s m t -> p (s m t)"))
 
-        w_columns = w_raw[:].rearrange("p t h -> p h t")
-
         def group_w(copy, half, first, end):
-            src = w_columns[:, HALF * half + first : HALF * half + end]
+            src = w_raw[:].rearrange("p t h -> p h t")[:, HALF * half + first : HALF * half + end]
             copy(w_grouped[half].rearrange("p (h t) -> p h t", t=PACK)[:, first:end], src)
 
         def quantize_w(half):
@@ -244,11 +242,13 @@ def tile_controencodnet_pa_kernel(tc, f_bytes, f_scale, x, w1, b1, out):
 
         pair_tanh = [keep.tile([P, PAIR * P], F32, name="pair_tanh%d" % j, align_bytes=64) for j in range(HID // P)]
 
+        pair_codes = keep.tile([P, PAIR * P], U32, name="pair_codes", align_bytes=64)
+        pair_scales = keep.tile([P, PAIR * P], U8, name="pair_scales", align_bytes=64)
+
+        def quantize_pair():
+            nc.vector.quantize_mx(out=pair_codes[:].bitcast(FP8X4), scales=pair_scales[:], in_=pair_grouped[:].rearrange("p b r s -> p (b r s)"))
+
         def pair_product(bias_columns):
-            codes = keep.tile([P, PAIR * P], U32, name="pair_codes", align_bytes=64)
-            scales = keep.tile([P, PAIR * P], U8, name="pair_scales", align_bytes=64)
-            nc.vector.quantize_mx(out=codes[:].bitcast(FP8X4), scales=scales[:], in_=pair_grouped[:].rearrange("p b r s -> p (b r s)"))
-            quantize_w(1)
             banks = [bank(number) for number in range(PAIR)]
             tiles = [banks[j // 2][:, (j % 2) * PAIR * P : (j % 2 + 1) * PAIR * P] for j in range(HID // P)]
             for j, tile in enumerate(tiles):
@@ -257,8 +257,8 @@ def tile_controencodnet_pa_kernel(tc, f_bytes, f_scale, x, w1, b1, out):
                     out=tile,
                     lhsT=w_codes[:, cols].bitcast(FP8X4),
                     lhsT_scale=w_scales[:, cols],
-                    rhs=codes[:].bitcast(FP8X4),
-                    rhs_scale=scales[:],
+                    rhs=pair_codes[:].bitcast(FP8X4),
+                    rhs_scale=pair_scales[:],
                     start=True,
                     stop=True,
                 )
@@ -266,13 +266,13 @@ def tile_controencodnet_pa_kernel(tc, f_bytes, f_scale, x, w1, b1, out):
                 nc.scalar.activation(out=pair_tanh[j][:], in_=tile, func=ACT.Tanh, bias=bias_columns[:, j : j + 1])
 
         def turn_back(b):
-            second[b] = bank(b)
+            back[b] = bank(b)
             for j in range(HID // P):
-                nc.tensor.transpose(second[b][:, j * P : (j + 1) * P], pair_tanh[j][:, b * P : (b + 1) * P], identity[:])
+                nc.tensor.transpose(back[b][:, j * P : (j + 1) * P], pair_tanh[j][:, b * P : (b + 1) * P], identity[:])
 
         def store_turned(b):
             result[b] = each.tile([P, HID], F32, name="result")
-            nc.scalar.copy(out=result[b][:], in_=second[b][:])
+            nc.scalar.copy(out=result[b][:], in_=back[b][:])
             nc.sync.dma_start(out=out_view[:, b, :], in_=result[b][:])
 
         def scalar_copy(dst, src):
@@ -283,27 +283,28 @@ def tile_controencodnet_pa_kernel(tc, f_bytes, f_scale, x, w1, b1, out):
 
         warm = bank(6)
         for unused in range(2):
-            warm_up(224, warm)
+            warm_up(WARM_FIRST, warm)
+
         first_block()
-        for b in range(1, 4):
-            widen(b)
-            turn(b)
-            if b != 2:
-                warm_up(256, warm)
-            scale_out(b)
+        for blocks in ((1,), (2, 3)):
+            for b in blocks:
+                widen(b)
+                turn(b)
+                scale_out(b)
+            warm_up(WARM_BETWEEN, warm)
         group_x(gpsimd_copy, 0, 0, X_TILES_ON_GPSIMD)
         group_x(scalar_copy, 0, X_TILES_ON_GPSIMD, PACK)
-        widen(4)
-        widen(5)
+        for b in (4, 5):
+            widen(b)
 
-        group_x(scalar_copy, 1, 2, PACK)
-        scalar_copy(x_tiles(1, 0, 2), group_x_on_tensor(1, 0, 2, 0))
-        turn(4)
-        turn(5)
+        group_x(scalar_copy, 1, X_TILES_ON_TENSOR, PACK)
+        group_x_on_tensor(1, X_TILES_ON_TENSOR, 0)
+        for b in (4, 5):
+            turn(b)
 
-        bias_turned = bank(2, BF16, 2 * 512)
+        bias_turned = bank(2, BF16, 2 * BANK)
         nc.tensor.transpose(bias_turned[:, :P], bias_rows[:], identity_bf[:])
-        warm_up(256, warm)
+        warm_up(WARM_BETWEEN, warm)
 
         widen(6)
         group_w(scalar_copy, 0, 0, HALF)
@@ -312,30 +313,32 @@ def tile_controencodnet_pa_kernel(tc, f_bytes, f_scale, x, w1, b1, out):
         bias_columns = keep.tile([P, HID // P], F32, name="bias_columns")
         nc.scalar.copy(out=bias_columns[:], in_=bias_turned[:, : HID // P])
 
-        quantize_x(0)
-        quantize_f(0, 2)
-        quantize_x(1)
-        quantize_f(2, 2)
+        for g in range(PASSES):
+            quantize_x(g)
+            quantize_f(2 * g, 2)
 
         group_w(gpsimd_copy, 1, 0, W_COLS_ON_GPSIMD)
         group_w(scalar_copy, 1, W_COLS_ON_GPSIMD, HALF)
-        scale_out(4)
-        scale_out(5)
+        for b in (4, 5):
+            scale_out(b)
         quantize_f(4)
         for b in range(5):
             first_product(b)
             copy_agg(b)
+
         quantize_w(0)
+        quantize_pair()
+        quantize_w(1)
         pair_product(bias_columns)
 
-        quantize_agg(2)
         quantize_f(5)
+        quantize_agg(2)
         second_product(2)
         first_product(5)
         turn(LAST)
         scale_out(6)
-        add_bias(2)
         quantize_agg(3)
+        add_bias(2)
         quantize_f(6)
         copy_agg(5)
         finish(2)
@@ -346,8 +349,8 @@ def tile_controencodnet_pa_kernel(tc, f_bytes, f_scale, x, w1, b1, out):
         copy_agg(6)
         store_turned(1)
         scale_out(LAST)
-        quantize_agg(4)
-        quantize_agg(5)
+        for b in (4, 5):
+            quantize_agg(b)
         quantize_f(LAST)
 
         for b in range(3, 6):
@@ -357,7 +360,7 @@ def tile_controencodnet_pa_kernel(tc, f_bytes, f_scale, x, w1, b1, out):
         finish(3)
         quantize_agg(6)
         second_product(6)
-        warm_up(128, bank(1))
+        warm_up(WARM_LAST, bank(1))
         copy_agg(LAST)
         for b in range(4, LAST):
             add_bias(b)

@@ -71,10 +71,10 @@ def tile_controencodnet_pa_kernel(tc, f_bytes, f_scale, x, w1, b1, out):
         raw = {}
 
         def load_f(first, count):
-            tile = keep.tile([P, count, NODES], U8, name="f_raw%d" % first)
-            nc.sync.dma_start(out=tile[:], in_=f_view[:, first : first + count, :])
+            loaded = keep.tile([P, count, NODES], U8, name="f_raw%d" % first)
+            nc.sync.dma_start(out=loaded[:], in_=f_view[:, first : first + count, :])
             for j in range(count):
-                raw[first + j] = tile[:, j, :]
+                raw[first + j] = loaded[:, j, :]
 
         x_raw = [keep.tile([P, PACK, FEATS], BF16, name="x_raw%d" % g) for g in range(PASSES)]
         w_raw = keep.tile([P, PACK, HID], BF16, name="w_raw")
@@ -144,11 +144,11 @@ def tile_controencodnet_pa_kernel(tc, f_bytes, f_scale, x, w1, b1, out):
                 nc.vector.tensor_copy(out=wide[0][:, cols], in_=raw[0][:, cols].bitcast(FP8))
             scaled[0] = scaled_tile(0)
             for g, number in enumerate((0, LAST)):
-                half = bank(number)
-                turn_pass(lambda u: half[:, u * P : (u + 1) * P], 0, g)
+                pass_bank = bank(number)
+                turn_pass(lambda u: pass_bank[:, u * P : (u + 1) * P], 0, g)
                 nc.vector.tensor_tensor(
                     out=scaled[0].rearrange("p (g r u e) -> p g r u e", g=PASSES, u=2, e=2)[:, g],
-                    in0=half[:, : 2 * P].bitcast(BF16).rearrange("p (u r e) -> p r u e", u=2, e=2),
+                    in0=pass_bank[:, : 2 * P].bitcast(BF16).rearrange("p (u r e) -> p r u e", u=2, e=2),
                     in1=scale[:, g].rearrange("p (u e) -> p u e", e=2).unsqueeze(1).to_broadcast([P, P, 2, 2]),
                     op=ALU.mult,
                 )
@@ -331,8 +331,8 @@ def tile_controencodnet_pa_kernel(tc, f_bytes, f_scale, x, w1, b1, out):
         quantize_w(1)
         pair_product(bias_columns)
 
-        quantize_f(5)
         quantize_agg(2)
+        quantize_f(5)
         second_product(2)
         first_product(5)
         turn(LAST)

@@ -27,10 +27,12 @@ BANK = 512
 LAST = BLOCKS - 1
 
 X_TILES_ON_GPSIMD = 3
-W_COLS_ON_GPSIMD = 192
+W_COLS_ON_GPSIMD = 256
 X_TILES_ON_TENSOR = 2
 
-WARM_FIRST = 224
+WARM_FIRST = 192
+WARM_SHORT = 160
+WARM_LATE = 192
 WARM_BETWEEN = 256
 WARM_LAST = 128
 
@@ -80,7 +82,9 @@ def tile_controencodnet_pa_kernel(tc, f_bytes, f_scale, x, w1, b1, out):
         w_raw = keep.tile([P, PACK, HID], BF16, name="w_raw")
         bias = keep.tile([P, HID], BF16, name="bias")
 
-        load_f(0, 1)
+        first_raw = [keep.tile([P, K_PASS], U8, name="f_first%d" % g) for g in range(PASSES)]
+        for g in range(PASSES):
+            nc.sync.dma_start(out=first_raw[g][:], in_=f_view[:, 0, g * K_PASS : (g + 1) * K_PASS])
         load_f(1, 1)
         scale = keep.tile([P, PASSES, PACK], F32, name="scale")
         nc.sync.dma_start(out=scale[:], in_=f_scale.rearrange("o (g p t) -> p (o g) t", p=P, t=PACK))
@@ -95,7 +99,6 @@ def tile_controencodnet_pa_kernel(tc, f_bytes, f_scale, x, w1, b1, out):
         nc.sync.dma_start(out=bias[:], in_=b1.partition_broadcast(P))
 
         identity_bf = keep.tile([P, P], BF16, name="identity_bf")
-        nc.vector.tensor_copy(out=identity_bf[:], in_=identity[:])
 
         x_grouped = [keep.tile([P, PACK, P, PACK], BF16, name="x_grouped%d" % g, align_bytes=64) for g in range(PASSES)]
         x_codes = [keep.tile([P, FEATS], U32, name="x_codes%d" % g, align_bytes=64) for g in range(PASSES)]
@@ -140,8 +143,8 @@ def tile_controencodnet_pa_kernel(tc, f_bytes, f_scale, x, w1, b1, out):
         def first_block():
             wide[0] = each.tile([P, NODES], BF16, name="wide", align_bytes=64)
             for g in range(PASSES):
-                cols = slice(g * K_PASS, (g + 1) * K_PASS)
-                nc.vector.tensor_copy(out=wide[0][:, cols], in_=raw[0][:, cols].bitcast(FP8))
+                nc.vector.tensor_copy(out=wide[0][:, g * K_PASS : (g + 1) * K_PASS], in_=first_raw[g][:].bitcast(FP8))
+            nc.vector.tensor_copy(out=identity_bf[:], in_=identity[:])
             scaled[0] = scaled_tile(0)
             for g, number in enumerate((0, LAST)):
                 pass_bank = bank(number)
@@ -291,7 +294,7 @@ def tile_controencodnet_pa_kernel(tc, f_bytes, f_scale, x, w1, b1, out):
                 widen(b)
                 turn(b)
                 scale_out(b)
-            warm_up(WARM_BETWEEN, warm)
+            warm_up(WARM_SHORT if blocks == (1,) else WARM_BETWEEN, warm)
         group_x(gpsimd_copy, 0, 0, X_TILES_ON_GPSIMD)
         group_x(scalar_copy, 0, X_TILES_ON_GPSIMD, PACK)
         for b in (4, 5):
@@ -304,7 +307,7 @@ def tile_controencodnet_pa_kernel(tc, f_bytes, f_scale, x, w1, b1, out):
 
         bias_turned = bank(2, BF16, 2 * BANK)
         nc.tensor.transpose(bias_turned[:, :P], bias_rows[:], identity_bf[:])
-        warm_up(WARM_BETWEEN, warm)
+        warm_up(WARM_LATE, bank(LAST))
 
         widen(6)
         group_w(scalar_copy, 0, 0, HALF)
@@ -318,7 +321,6 @@ def tile_controencodnet_pa_kernel(tc, f_bytes, f_scale, x, w1, b1, out):
             quantize_f(2 * g, 2)
 
         group_w(gpsimd_copy, 1, 0, W_COLS_ON_GPSIMD)
-        group_w(scalar_copy, 1, W_COLS_ON_GPSIMD, HALF)
         for b in (4, 5):
             scale_out(b)
         quantize_f(4)

@@ -27,13 +27,12 @@ BANK = 512
 LAST = BLOCKS - 1
 
 X_TILES_ON_GPSIMD = 3
-W_COLS_ON_GPSIMD = 256
 X_TILES_ON_TENSOR = 2
 
 WARM_FIRST = 192
+WARM_TINY = 32
 WARM_SHORT = 160
-WARM_LATE = 192
-WARM_BETWEEN = 256
+WARM_BETWEEN = 192
 WARM_LAST = 128
 
 
@@ -107,7 +106,7 @@ def tile_controencodnet_pa_kernel(tc, f_bytes, f_scale, x, w1, b1, out):
         w_scales = keep.tile([P, HID], U8, name="w_scales", align_bytes=64)
 
         scaled_pair = [keep.tile([P, 2 * NODES], BF16, name="scaled_pair%d" % n, align_bytes=64) for n in range(2)]
-        w_grouped = [keep.tile([P, PACK * HALF], BF16, name="w_grouped", align_bytes=64)[:], scaled_pair[1][:, NODES:]]
+        w_grouped = [keep.tile([P, PACK * HALF], BF16, name="w_grouped", align_bytes=64)[:], x_grouped[1][:, :2].rearrange("p s m t -> p (s m t)")]
 
         wide, turned, scaled, f_mx, agg, agg_grouped, agg_mx, second, back, biased, result = ({} for unused in range(11))
 
@@ -289,6 +288,7 @@ def tile_controencodnet_pa_kernel(tc, f_bytes, f_scale, x, w1, b1, out):
             warm_up(WARM_FIRST, warm)
 
         first_block()
+        warm_up(WARM_TINY, warm)
         for blocks in ((1,), (2, 3)):
             for b in blocks:
                 widen(b)
@@ -307,7 +307,7 @@ def tile_controencodnet_pa_kernel(tc, f_bytes, f_scale, x, w1, b1, out):
 
         bias_turned = bank(2, BF16, 2 * BANK)
         nc.tensor.transpose(bias_turned[:, :P], bias_rows[:], identity_bf[:])
-        warm_up(WARM_LATE, bank(LAST))
+        warm_up(WARM_BETWEEN, bank(LAST))
 
         widen(6)
         group_w(scalar_copy, 0, 0, HALF)
@@ -320,7 +320,7 @@ def tile_controencodnet_pa_kernel(tc, f_bytes, f_scale, x, w1, b1, out):
             quantize_x(g)
             quantize_f(2 * g, 2)
 
-        group_w(gpsimd_copy, 1, 0, W_COLS_ON_GPSIMD)
+        group_w(gpsimd_copy, 1, 0, HALF)
         for b in (4, 5):
             scale_out(b)
         quantize_f(4)

@@ -26,9 +26,10 @@ HALF = HID // 2
 BANK = 512
 LAST = BLOCKS - 1
 
-X_TILES_ON_GPSIMD = 3
+X_RUNS_ON_GPSIMD = 14
 X_TILES_ON_TENSOR = 2
 
+FIRST_ON_VECTOR = 320
 WARM_FIRST = 192
 WARM_TINY = 32
 WARM_SHORT = 160
@@ -58,10 +59,8 @@ def tile_controencodnet_pa_kernel(tc, f_bytes, f_scale, x, w1, b1, out):
         zeros = keep.tile([P, WARM_BETWEEN], F32, name="zeros")
         nc.vector.memset(zeros[:], 0.0)
 
-        table_in = keep.tile([P, 1], F32, name="table_in")
         table_out = keep.tile([P, 1], F32, name="table_out")
-        nc.vector.memset(table_in[:], 0.0)
-        nc.scalar.activation(out=table_out[:], in_=table_in[:], func=ACT.Tanh)
+        nc.scalar.activation(out=table_out[:], in_=zeros[:, :1], func=ACT.Tanh)
 
         identity = keep.tile([P, P], F32, name="identity")
         make_identity(nc, identity[:])
@@ -99,16 +98,20 @@ def tile_controencodnet_pa_kernel(tc, f_bytes, f_scale, x, w1, b1, out):
 
         identity_bf = keep.tile([P, P], BF16, name="identity_bf")
 
-        x_grouped = [keep.tile([P, PACK, P, PACK], BF16, name="x_grouped%d" % g, align_bytes=64) for g in range(PASSES)]
-        x_codes = [keep.tile([P, FEATS], U32, name="x_codes%d" % g, align_bytes=64) for g in range(PASSES)]
-        x_scales = [keep.tile([P, FEATS], U8, name="x_scales%d" % g, align_bytes=64) for g in range(PASSES)]
+        x_width = PACK * FEATS
+        x0_and_blocks = keep.tile([P, x_width + PAIR * NODES], BF16, name="x0_and_blocks", align_bytes=64)
+        first_codes = keep.tile([P, FEATS + PAIR * PASSES * P], U32, name="first_codes", align_bytes=64)
+        first_scales = keep.tile([P, FEATS + PAIR * PASSES * P], U8, name="first_scales", align_bytes=64)
+        x_grouped = [x0_and_blocks[:, :x_width], keep.tile([P, x_width], BF16, name="x1_grouped", align_bytes=64)[:]]
+        w_grouped = [keep.tile([P, PACK * HALF], BF16, name="w_grouped%d" % half, align_bytes=64)[:] for half in range(2)]
+        x_codes = [first_codes[:, :FEATS], keep.tile([P, FEATS], U32, name="x1_codes", align_bytes=64)[:]]
+        x_scales = [first_scales[:, :FEATS], keep.tile([P, FEATS], U8, name="x1_scales", align_bytes=64)[:]]
         w_codes = keep.tile([P, HID], U32, name="w_codes", align_bytes=64)
         w_scales = keep.tile([P, HID], U8, name="w_scales", align_bytes=64)
+        scaled_pair = [x0_and_blocks[:, x_width:], keep.tile([P, PAIR * NODES], BF16, name="scaled_pair", align_bytes=64)[:]]
 
-        scaled_pair = [keep.tile([P, 2 * NODES], BF16, name="scaled_pair%d" % n, align_bytes=64) for n in range(2)]
-        w_grouped = [keep.tile([P, PACK * HALF], BF16, name="w_grouped", align_bytes=64)[:], x_grouped[1][:, :2].rearrange("p s m t -> p (s m t)")]
-
-        wide, turned, scaled, f_mx, agg, agg_grouped, agg_mx, second, back, biased, result = ({} for unused in range(11))
+        plain = {}
+        wide, turned, scaled, f_mx, agg, agg_mx, second, back, biased, result = ({} for unused in range(10))
 
         def widen(b):
             wide[b] = each.tile([P, NODES], BF16, name="wide", align_bytes=64)
@@ -141,8 +144,9 @@ def tile_controencodnet_pa_kernel(tc, f_bytes, f_scale, x, w1, b1, out):
 
         def first_block():
             wide[0] = each.tile([P, NODES], BF16, name="wide", align_bytes=64)
-            for g in range(PASSES):
-                nc.vector.tensor_copy(out=wide[0][:, g * K_PASS : (g + 1) * K_PASS], in_=first_raw[g][:].bitcast(FP8))
+            nc.vector.tensor_copy(out=wide[0][:, :FIRST_ON_VECTOR], in_=first_raw[0][:, :FIRST_ON_VECTOR].bitcast(FP8))
+            nc.scalar.copy(out=wide[0][:, FIRST_ON_VECTOR:K_PASS], in_=first_raw[0][:, FIRST_ON_VECTOR:].bitcast(FP8))
+            nc.vector.tensor_copy(out=wide[0][:, K_PASS:], in_=first_raw[1][:].bitcast(FP8))
             nc.vector.tensor_copy(out=identity_bf[:], in_=identity[:])
             scaled[0] = scaled_tile(0)
             for g, number in enumerate((0, LAST)):
@@ -155,32 +159,61 @@ def tile_controencodnet_pa_kernel(tc, f_bytes, f_scale, x, w1, b1, out):
                     op=ALU.mult,
                 )
 
+        def copy_turned(b):
+            plain[b] = keep.tile([P, PASSES, P, PACK], BF16, name="plain%d" % b, align_bytes=64)
+            nc.scalar.copy(
+                out=plain[b][:].rearrange("p g r t -> p (g r t)").bitcast(F32).rearrange("p (m u) -> p m u", u=2),
+                in_=turned[b][:].rearrange("p (u m) -> p m u", u=2),
+            )
+
+        def scale_on_gpsimd(b, place):
+            scaled[b] = place
+            nc.gpsimd.tensor_tensor(
+                out=place.rearrange("p (g r t) -> p g r t", g=PASSES, t=PACK),
+                in0=plain[b][:],
+                in1=scale[:].unsqueeze(2).to_broadcast([P, PASSES, P, PACK]),
+                op=ALU.mult,
+            )
+
         def quantize_f(first, count=1):
             width = PASSES * P
             codes = keep.tile([P, count * width], U32, name="f_codes%d" % first, align_bytes=64)
             scales = keep.tile([P, count * width], U8, name="f_scales%d" % first, align_bytes=64)
-            source = scaled[first] if count == 1 else scaled_pair[first // 2][:]
+            source = scaled[first] if count == 1 else scaled_pair[first // 2]
             nc.vector.quantize_mx(out=codes[:].bitcast(FP8X4), scales=scales[:], in_=source)
             for j in range(count):
                 f_mx[first + j] = (codes[:, j * width : (j + 1) * width], scales[:, j * width : (j + 1) * width])
 
-        def group_x(copy, g, first, end):
-            dst = x_grouped[g][:].rearrange("p s (a i) t -> p a s i t", i=RUN)[:, :, first:end]
-            copy(dst, x_raw[g][:].rearrange("p t (a s i) -> p a s i t", s=PACK, i=RUN)[:, :, first:end])
+        def group_x(copy, g, tiles=slice(0, PACK), runs=slice(0, P // RUN)):
+            dst = x_grouped[g].rearrange("p (s a i t) -> p a s i t", s=PACK, i=RUN, t=PACK)[:, runs, tiles]
+            copy(dst, x_raw[g][:].rearrange("p t (a s i) -> p a s i t", s=PACK, i=RUN)[:, runs, tiles])
 
         def group_x_on_tensor(g, count, number):
             tiles = x_raw[g][:].rearrange("p t (a s i) -> p s a i t", s=PACK, i=RUN)
             held = bank(number, BF16, 2 * BANK)
             for s in range(count):
                 nc.tensor.matmul(out=held[:, s * BANK : (s + 1) * BANK], lhsT=identity_bf[:], rhs=tiles[:, s], start=True, stop=True)
-            nc.scalar.copy(out=x_grouped[g][:, :count].rearrange("p s m t -> p (s m t)"), in_=held[:, : count * BANK])
+            nc.scalar.copy(out=x_grouped[g][:, : count * BANK], in_=held[:, : count * BANK])
 
-        def quantize_x(g):
-            nc.vector.quantize_mx(out=x_codes[g][:].bitcast(FP8X4), scales=x_scales[g][:], in_=x_grouped[g][:].rearrange("p s m t -> p (s m t)"))
+        def quantize_x0_and_blocks():
+            nc.vector.quantize_mx(out=first_codes[:].bitcast(FP8X4), scales=first_scales[:], in_=x0_and_blocks[:])
+            for b in range(PAIR):
+                cols = slice(FEATS + b * PASSES * P, FEATS + (b + 1) * PASSES * P)
+                f_mx[b] = (first_codes[:, cols], first_scales[:, cols])
 
-        def group_w(copy, half, first, end):
-            src = w_raw[:].rearrange("p t h -> p h t")[:, HALF * half + first : HALF * half + end]
-            copy(w_grouped[half].rearrange("p (h t) -> p h t", t=PACK)[:, first:end], src)
+        def quantize_x1():
+            nc.vector.quantize_mx(out=x_codes[1].bitcast(FP8X4), scales=x_scales[1], in_=x_grouped[1])
+
+        def group_w(copy, half):
+            cols = slice(HALF * half, HALF * (half + 1))
+            copy(w_grouped[half].rearrange("p (h t) -> p h t", t=PACK), w_raw[:].rearrange("p t h -> p h t")[:, cols])
+
+        def group_w_on_tensor(half, number):
+            rows = w_raw[:].rearrange("p t h -> p h t")
+            held = bank(number, BF16, 2 * BANK)
+            for q in range(2):
+                nc.tensor.matmul(out=held[:, q * BANK : (q + 1) * BANK], lhsT=identity_bf[:], rhs=rows[:, HALF * half + q * P : HALF * half + (q + 1) * P], start=True, stop=True)
+            return lambda: nc.scalar.copy(out=w_grouped[half], in_=held[:])
 
         def quantize_w(half):
             cols = slice(HALF * half, HALF * (half + 1))
@@ -203,28 +236,27 @@ def tile_controencodnet_pa_kernel(tc, f_bytes, f_scale, x, w1, b1, out):
                         stop=(g == PASSES - 1),
                     )
 
-        pair_grouped = keep.tile([P, PAIR, P, PACK], BF16, name="pair_grouped", align_bytes=64)
+        agg_pair = [keep.tile([P, PAIR, P, PACK], BF16, name="agg_pair%d" % n, align_bytes=64) for n in range(BLOCKS // PAIR)]
 
         def copy_agg(b):
-            if b < PAIR:
-                agg_grouped[b] = pair_grouped[:, b]
-            else:
-                agg_grouped[b] = each.tile([P, P, PACK], BF16, name="agg_grouped", align_bytes=64)[:]
-            nc.scalar.copy(out=agg_grouped[b], in_=agg[b][:].rearrange("p (s r) -> p r s", s=PACK))
+            nc.scalar.copy(out=agg_pair[b // PAIR][:, b % PAIR], in_=agg[b][:].rearrange("p (s r) -> p r s", s=PACK))
 
-        def quantize_agg(b):
-            codes = each.tile([P, P], U32, name="agg_codes", align_bytes=64)
-            scales = each.tile([P, P], U8, name="agg_scales", align_bytes=64)
-            nc.vector.quantize_mx(out=codes[:].bitcast(FP8X4), scales=scales[:], in_=agg_grouped[b].rearrange("p r s -> p (r s)"))
-            agg_mx[b] = (codes, scales)
+        def quantize_agg(first, count=1):
+            codes = keep.tile([P, count * P], U32, name="agg_codes%d" % first, align_bytes=64)
+            scales = keep.tile([P, count * P], U8, name="agg_scales%d" % first, align_bytes=64)
+            source = agg_pair[first // PAIR][:, first % PAIR : first % PAIR + count].rearrange("p b r s -> p (b r s)")
+            nc.vector.quantize_mx(out=codes[:].bitcast(FP8X4), scales=scales[:], in_=source)
+            for j in range(count):
+                agg_mx[first + j] = (codes[:, j * P : (j + 1) * P], scales[:, j * P : (j + 1) * P])
+            return codes, scales
 
         def second_product(b, cols=slice(0, HID), number=None):
             codes, scales = agg_mx[b]
             second[b, cols.start] = bank(b if number is None else number)[:, cols]
             nc.tensor.matmul_mx(
                 out=second[b, cols.start],
-                lhsT=codes[:].bitcast(FP8X4),
-                lhsT_scale=scales[:],
+                lhsT=codes.bitcast(FP8X4),
+                lhsT_scale=scales,
                 rhs=w_codes[:, cols].bitcast(FP8X4),
                 rhs_scale=w_scales[:, cols],
                 start=True,
@@ -244,13 +276,7 @@ def tile_controencodnet_pa_kernel(tc, f_bytes, f_scale, x, w1, b1, out):
 
         pair_tanh = [keep.tile([P, PAIR * P], F32, name="pair_tanh%d" % j, align_bytes=64) for j in range(HID // P)]
 
-        pair_codes = keep.tile([P, PAIR * P], U32, name="pair_codes", align_bytes=64)
-        pair_scales = keep.tile([P, PAIR * P], U8, name="pair_scales", align_bytes=64)
-
-        def quantize_pair():
-            nc.vector.quantize_mx(out=pair_codes[:].bitcast(FP8X4), scales=pair_scales[:], in_=pair_grouped[:].rearrange("p b r s -> p (b r s)"))
-
-        def pair_product(bias_columns):
+        def pair_product(pair_codes, pair_scales, bias_columns):
             banks = [bank(number) for number in range(PAIR)]
             tiles = [banks[j // 2][:, (j % 2) * PAIR * P : (j % 2 + 1) * PAIR * P] for j in range(HID // P)]
             for j, tile in enumerate(tiles):
@@ -272,9 +298,9 @@ def tile_controencodnet_pa_kernel(tc, f_bytes, f_scale, x, w1, b1, out):
             for j in range(HID // P):
                 nc.tensor.transpose(back[b][:, j * P : (j + 1) * P], pair_tanh[j][:, b * P : (b + 1) * P], identity[:])
 
-        def store_turned(b):
+        def store_turned(b, copy):
             result[b] = each.tile([P, HID], F32, name="result")
-            nc.scalar.copy(out=result[b][:], in_=back[b][:])
+            copy(out=result[b][:], in_=back[b][:])
             nc.sync.dma_start(out=out_view[:, b, :], in_=result[b][:])
 
         def scalar_copy(dst, src):
@@ -286,7 +312,6 @@ def tile_controencodnet_pa_kernel(tc, f_bytes, f_scale, x, w1, b1, out):
         warm = bank(6)
         for unused in range(2):
             warm_up(WARM_FIRST, warm)
-
         first_block()
         warm_up(WARM_TINY, warm)
         for blocks in ((1,), (2, 3)):
@@ -295,83 +320,79 @@ def tile_controencodnet_pa_kernel(tc, f_bytes, f_scale, x, w1, b1, out):
                 turn(b)
                 scale_out(b)
             warm_up(WARM_SHORT if blocks == (1,) else WARM_BETWEEN, warm)
-        group_x(gpsimd_copy, 0, 0, X_TILES_ON_GPSIMD)
-        group_x(scalar_copy, 0, X_TILES_ON_GPSIMD, PACK)
+        group_x(gpsimd_copy, 0, runs=slice(0, X_RUNS_ON_GPSIMD))
+        group_x(scalar_copy, 0, runs=slice(X_RUNS_ON_GPSIMD, P // RUN))
         for b in (4, 5):
             widen(b)
-
-        group_x(scalar_copy, 1, X_TILES_ON_TENSOR, PACK)
+        group_x(scalar_copy, 1, tiles=slice(X_TILES_ON_TENSOR, PACK))
         group_x_on_tensor(1, X_TILES_ON_TENSOR, 0)
         for b in (4, 5):
             turn(b)
-
         bias_turned = bank(2, BF16, 2 * BANK)
         nc.tensor.transpose(bias_turned[:, :P], bias_rows[:], identity_bf[:])
-        warm_up(WARM_BETWEEN, bank(LAST))
-
+        empty_w = group_w_on_tensor(0, LAST)
         widen(6)
-        group_w(scalar_copy, 0, 0, HALF)
         turn(6)
+        copy_turned(5)
         widen(LAST)
+        empty_w()
         bias_columns = keep.tile([P, HID // P], F32, name="bias_columns")
         nc.scalar.copy(out=bias_columns[:], in_=bias_turned[:, : HID // P])
-
-        for g in range(PASSES):
-            quantize_x(g)
-            quantize_f(2 * g, 2)
-
-        group_w(gpsimd_copy, 1, 0, HALF)
-        for b in (4, 5):
+        group_w(scalar_copy, 1)
+        quantize_x0_and_blocks()
+        quantize_x1()
+        quantize_f(2, PAIR)
+        scale_on_gpsimd(5, x_grouped[1][:, :NODES])
+        for b in (4, 6):
             scale_out(b)
         quantize_f(4)
         for b in range(5):
+            if b == 4:
+                turn(LAST)
             first_product(b)
             copy_agg(b)
-
         quantize_w(0)
-        quantize_pair()
+        pair_codes, pair_scales = quantize_agg(0, PAIR)
         quantize_w(1)
-        pair_product(bias_columns)
-
-        quantize_agg(2)
+        pair_product(pair_codes, pair_scales, bias_columns)
         quantize_f(5)
-        second_product(2)
+        quantize_agg(2)
+        quantize_f(6)
         first_product(5)
-        turn(LAST)
-        scale_out(6)
+        second_product(2)
+        first_product(6)
+        scale_out(LAST)
         quantize_agg(3)
         add_bias(2)
-        quantize_f(6)
+        quantize_f(LAST)
+        quantize_agg(4)
         copy_agg(5)
+        copy_agg(6)
         finish(2)
         for b in range(PAIR):
             turn_back(b)
-        store_turned(0)
-        first_product(6)
-        copy_agg(6)
-        store_turned(1)
-        scale_out(LAST)
-        for b in (4, 5):
-            quantize_agg(b)
-        quantize_f(LAST)
-
-        for b in range(3, 6):
-            second_product(b)
+        second_product(3)
         first_product(LAST)
+        second_product(4)
+        store_turned(0, nc.vector.tensor_copy)
         add_bias(3)
-        finish(3)
+        quantize_agg(5)
         quantize_agg(6)
+        second_product(5)
         second_product(6)
-        warm_up(WARM_LAST, bank(1))
+        store_turned(1, nc.scalar.copy)
+        warm_up(WARM_LAST, bank(2))
         copy_agg(LAST)
-        for b in range(4, LAST):
+        finish(3)
+        for b in range(4, 6):
             add_bias(b)
             finish(b)
-
         quantize_agg(LAST)
         halves = [slice(HALF * half, HALF * (half + 1)) for half in range(2)]
         for cols, number in zip(halves, (LAST, 0)):
             second_product(LAST, cols, number)
+        add_bias(6)
+        finish(6)
         for cols in halves:
             add_bias(LAST, cols)
             finish(LAST, cols)

@@ -20,14 +20,12 @@ PACK = 4
 BLOCKS = NODES // P
 PASSES = NODES // (P * PACK)
 K_PASS = P * PACK
-RUN = 8
 PAIR = 2
 HALF = HID // 2
 BANK = 512
 LAST = BLOCKS - 1
 
-X_RUNS_ON_GPSIMD = 14
-X_TILES_ON_TENSOR = 2
+X_COLUMNS_ON_GPSIMD = 448
 
 FIRST_ON_VECTOR = 320
 WARM_FIRST = 192
@@ -42,7 +40,7 @@ def tile_controencodnet_pa_kernel(tc, f_bytes, f_scale, x, w1, b1, out):
     f_view = f_bytes.rearrange("(r b) k -> r b k", b=BLOCKS)
     out_view = out.rearrange("(r b) h -> r b h", b=BLOCKS)
     x_view = x.rearrange("(g p t) c -> g p t c", p=P, t=PACK)
-    w_view = w1.rearrange("(a t i) h -> t a i h", t=PACK, i=RUN)
+    w_view = w1.rearrange("(p t) h -> p t h", t=PACK)
 
     with ExitStack() as ctx:
         keep = ctx.enter_context(tc.tile_pool(name="keep", bufs=1))
@@ -90,10 +88,9 @@ def tile_controencodnet_pa_kernel(tc, f_bytes, f_scale, x, w1, b1, out):
         nc.sync.dma_start(out=x_raw[0][:], in_=x_view[0])
         load_f(4, 2)
         nc.sync.dma_start(out=x_raw[1][:], in_=x_view[1])
-        nc.sync.dma_start(out=bias_rows[0 : HID // P, :], in_=b1.rearrange("(j p) -> j p", p=P))
         load_f(6, 2)
-        for t in range(PACK):
-            nc.sync.dma_start(out=w_raw[:, t, :], in_=w_view[t])
+        nc.sync.dma_start(out=bias_rows[0 : HID // P, :], in_=b1.rearrange("(j p) -> j p", p=P))
+        nc.sync.dma_start(out=w_raw[:], in_=w_view)
         nc.sync.dma_start(out=bias[:], in_=b1.partition_broadcast(P))
 
         identity_bf = keep.tile([P, P], BF16, name="identity_bf")
@@ -184,16 +181,21 @@ def tile_controencodnet_pa_kernel(tc, f_bytes, f_scale, x, w1, b1, out):
             for j in range(count):
                 f_mx[first + j] = (codes[:, j * width : (j + 1) * width], scales[:, j * width : (j + 1) * width])
 
-        def group_x(copy, g, tiles=slice(0, PACK), runs=slice(0, P // RUN)):
-            dst = x_grouped[g].rearrange("p (s a i t) -> p a s i t", s=PACK, i=RUN, t=PACK)[:, runs, tiles]
-            copy(dst, x_raw[g][:].rearrange("p t (a s i) -> p a s i t", s=PACK, i=RUN)[:, runs, tiles])
+        def x_place(g, cols):
+            return x_grouped[g].rearrange("p (s m t) -> p m s t", s=PACK, t=PACK)[:, cols.start // PACK : cols.stop // PACK]
 
-        def group_x_on_tensor(g, count, number):
-            tiles = x_raw[g][:].rearrange("p t (a s i) -> p s a i t", s=PACK, i=RUN)
+        def group_x(copy, g, cols):
+            copy(x_place(g, cols), x_raw[g][:, :, cols].rearrange("p t (m s) -> p m s t", s=PACK))
+
+        def group_on_tensor(rows, first, number):
             held = bank(number, BF16, 2 * BANK)
-            for s in range(count):
-                nc.tensor.matmul(out=held[:, s * BANK : (s + 1) * BANK], lhsT=identity_bf[:], rhs=tiles[:, s], start=True, stop=True)
-            nc.scalar.copy(out=x_grouped[g][:, : count * BANK], in_=held[:, : count * BANK])
+            columns = rows[:].rearrange("p t c -> p c t")
+            for q in range(2):
+                nc.tensor.matmul(out=held[:, q * BANK : (q + 1) * BANK], lhsT=identity_bf[:], rhs=columns[:, first + q * P : first + (q + 1) * P], start=True, stop=True)
+            return held
+
+        def empty_x(g, cols, held):
+            nc.scalar.copy(out=x_place(g, cols).rearrange("p m s t -> p s m t"), in_=held[:].rearrange("p (m s t) -> p s m t", s=PACK, t=PACK))
 
         def quantize_x0_and_blocks():
             nc.vector.quantize_mx(out=first_codes[:].bitcast(FP8X4), scales=first_scales[:], in_=x0_and_blocks[:])
@@ -208,12 +210,8 @@ def tile_controencodnet_pa_kernel(tc, f_bytes, f_scale, x, w1, b1, out):
             cols = slice(HALF * half, HALF * (half + 1))
             copy(w_grouped[half].rearrange("p (h t) -> p h t", t=PACK), w_raw[:].rearrange("p t h -> p h t")[:, cols])
 
-        def group_w_on_tensor(half, number):
-            rows = w_raw[:].rearrange("p t h -> p h t")
-            held = bank(number, BF16, 2 * BANK)
-            for q in range(2):
-                nc.tensor.matmul(out=held[:, q * BANK : (q + 1) * BANK], lhsT=identity_bf[:], rhs=rows[:, HALF * half + q * P : HALF * half + (q + 1) * P], start=True, stop=True)
-            return lambda: nc.scalar.copy(out=w_grouped[half], in_=held[:])
+        def empty_w(half, held):
+            nc.scalar.copy(out=w_grouped[half], in_=held[:])
 
         def quantize_w(half):
             cols = slice(HALF * half, HALF * (half + 1))
@@ -236,15 +234,15 @@ def tile_controencodnet_pa_kernel(tc, f_bytes, f_scale, x, w1, b1, out):
                         stop=(g == PASSES - 1),
                     )
 
-        agg_pair = [keep.tile([P, PAIR, P, PACK], BF16, name="agg_pair%d" % n, align_bytes=64) for n in range(BLOCKS // PAIR)]
+        agg_all = keep.tile([P, BLOCKS, P, PACK], BF16, name="agg_all", align_bytes=64)
 
         def copy_agg(b):
-            nc.scalar.copy(out=agg_pair[b // PAIR][:, b % PAIR], in_=agg[b][:].rearrange("p (s r) -> p r s", s=PACK))
+            nc.scalar.copy(out=agg_all[:, b], in_=agg[b][:].rearrange("p (s r) -> p r s", s=PACK))
 
         def quantize_agg(first, count=1):
             codes = keep.tile([P, count * P], U32, name="agg_codes%d" % first, align_bytes=64)
             scales = keep.tile([P, count * P], U8, name="agg_scales%d" % first, align_bytes=64)
-            source = agg_pair[first // PAIR][:, first % PAIR : first % PAIR + count].rearrange("p b r s -> p (b r s)")
+            source = agg_all[:, first : first + count].rearrange("p b r s -> p (b r s)")
             nc.vector.quantize_mx(out=codes[:].bitcast(FP8X4), scales=scales[:], in_=source)
             for j in range(count):
                 agg_mx[first + j] = (codes[:, j * P : (j + 1) * P], scales[:, j * P : (j + 1) * P])
@@ -320,22 +318,23 @@ def tile_controencodnet_pa_kernel(tc, f_bytes, f_scale, x, w1, b1, out):
                 turn(b)
                 scale_out(b)
             warm_up(WARM_SHORT if blocks == (1,) else WARM_BETWEEN, warm)
-        group_x(gpsimd_copy, 0, runs=slice(0, X_RUNS_ON_GPSIMD))
-        group_x(scalar_copy, 0, runs=slice(X_RUNS_ON_GPSIMD, P // RUN))
+        halves = [slice(HALF * half, HALF * (half + 1)) for half in range(2)]
+        group_x(gpsimd_copy, 0, slice(0, X_COLUMNS_ON_GPSIMD))
+        group_x(scalar_copy, 0, slice(X_COLUMNS_ON_GPSIMD, FEATS))
         for b in (4, 5):
             widen(b)
-        group_x(scalar_copy, 1, tiles=slice(X_TILES_ON_TENSOR, PACK))
-        group_x_on_tensor(1, X_TILES_ON_TENSOR, 0)
+        group_x(scalar_copy, 1, halves[1])
+        empty_x(1, halves[0], group_on_tensor(x_raw[1], 0, 0))
         for b in (4, 5):
             turn(b)
         bias_turned = bank(2, BF16, 2 * BANK)
         nc.tensor.transpose(bias_turned[:, :P], bias_rows[:], identity_bf[:])
-        empty_w = group_w_on_tensor(0, LAST)
+        w_held = group_on_tensor(w_raw, 0, LAST)
         widen(6)
         turn(6)
         copy_turned(5)
         widen(LAST)
-        empty_w()
+        empty_w(0, w_held)
         bias_columns = keep.tile([P, HID // P], F32, name="bias_columns")
         nc.scalar.copy(out=bias_columns[:], in_=bias_turned[:, : HID // P])
         group_w(scalar_copy, 1)
@@ -356,39 +355,37 @@ def tile_controencodnet_pa_kernel(tc, f_bytes, f_scale, x, w1, b1, out):
         quantize_w(1)
         pair_product(pair_codes, pair_scales, bias_columns)
         quantize_f(5)
-        quantize_agg(2)
         quantize_f(6)
+        quantize_agg(2, 2)
         first_product(5)
         second_product(2)
         first_product(6)
+        second_product(3)
         scale_out(LAST)
-        quantize_agg(3)
         add_bias(2)
         quantize_f(LAST)
         quantize_agg(4)
+        add_bias(3)
         copy_agg(5)
-        copy_agg(6)
         finish(2)
+        copy_agg(6)
         for b in range(PAIR):
             turn_back(b)
-        second_product(3)
         first_product(LAST)
         second_product(4)
-        store_turned(0, nc.vector.tensor_copy)
-        add_bias(3)
         quantize_agg(5)
-        quantize_agg(6)
         second_product(5)
+        store_turned(0, nc.vector.tensor_copy)
+        quantize_agg(6)
         second_product(6)
         store_turned(1, nc.scalar.copy)
-        warm_up(WARM_LAST, bank(2))
         copy_agg(LAST)
+        warm_up(WARM_LAST, bank(2))
         finish(3)
-        for b in range(4, 6):
+        for b in (4, 5):
             add_bias(b)
             finish(b)
         quantize_agg(LAST)
-        halves = [slice(HALF * half, HALF * (half + 1)) for half in range(2)]
         for cols, number in zip(halves, (LAST, 0)):
             second_product(LAST, cols, number)
         add_bias(6)

from contextlib import ExitStack

import concourse.mybir as mybir
from concourse.masks import make_identity

NODES, FEATS, HID = 1024, 512, 512
FLOPS = 2 * NODES * NODES * FEATS + 2 * NODES * FEATS * HID

F32 = mybir.dt.float32
BF16 = mybir.dt.bfloat16
U32 = mybir.dt.uint32
U8 = mybir.dt.uint8
FP8 = mybir.dt.float8_e4m3fn
FP8X4 = mybir.dt.float8_e4m3fn_x4
ACT = mybir.ActivationFunctionType
ALU = mybir.AluOpType

P = 128
PACK = 4
BLOCKS = NODES // P
PASSES = NODES // (P * PACK)
K_PASS = P * PACK
PAIR = 2
HALF = HID // 2
BANK = 512
LAST = BLOCKS - 1

X_COLUMNS_ON_GPSIMD = 448

FIRST_ON_VECTOR = 320
WARM_FIRST = 192
WARM_TINY = 32
WARM_SHORT = 160
WARM_BETWEEN = 192
WARM_LAST = 128


def tile_controencodnet_pa_kernel(tc, f_bytes, f_scale, x, w1, b1, out):
    nc = tc.nc
    f_view = f_bytes.rearrange("(r b) k -> r b k", b=BLOCKS)
    out_view = out.rearrange("(r b) h -> r b h", b=BLOCKS)
    x_view = x.rearrange("(g p t) c -> g p t c", p=P, t=PACK)
    w_view = w1.rearrange("(p t) h -> p t h", t=PACK)

    with ExitStack() as ctx:
        keep = ctx.enter_context(tc.tile_pool(name="keep", bufs=1))
        each = ctx.enter_context(tc.tile_pool(name="each", bufs=BLOCKS))
        psum = ctx.enter_context(tc.psum_pool(name="psum", bufs=1))
        ctx.enter_context(tc.manual_schedule())

        def bank(number, dtype=F32, columns=BANK):
            return psum.tile([P, columns], dtype, name="bank%d" % number)

        def gpsimd_copy(dst, src):
            nc.gpsimd.tensor_scalar(out=dst, in0=src, scalar1=1.0, scalar2=0.0, op0=ALU.mult, op1=ALU.add)

        zeros = keep.tile([P, WARM_BETWEEN], F32, name="zeros")
        nc.vector.memset(zeros[:], 0.0)

        table_out = keep.tile([P, 1], F32, name="table_out")
        nc.scalar.activation(out=table_out[:], in_=zeros[:, :1], func=ACT.Tanh)

        identity = keep.tile([P, P], F32, name="identity")
        make_identity(nc, identity[:])

        bias_rows = keep.tile([P, P], BF16, name="bias_rows")
        nc.vector.memset(bias_rows[:], 0.0)

        raw = {}

        def load_f(first, count):
            loaded = keep.tile([P, count, NODES], U8, name="f_raw%d" % first)
            nc.sync.dma_start(out=loaded[:], in_=f_view[:, first : first + count, :])
            for j in range(count):
                raw[first + j] = loaded[:, j, :]

        x_raw = [keep.tile([P, PACK, FEATS], BF16, name="x_raw%d" % g) for g in range(PASSES)]
        w_raw = keep.tile([P, PACK, HID], BF16, name="w_raw")
        bias = keep.tile([P, HID], BF16, name="bias")

        first_raw = [keep.tile([P, K_PASS], U8, name="f_first%d" % g) for g in range(PASSES)]
        for g in range(PASSES):
            nc.sync.dma_start(out=first_raw[g][:], in_=f_view[:, 0, g * K_PASS : (g + 1) * K_PASS])
        load_f(1, 1)
        scale = keep.tile([P, PASSES, PACK], F32, name="scale")
        nc.sync.dma_start(out=scale[:], in_=f_scale.rearrange("o (g p t) -> p (o g) t", p=P, t=PACK))
        load_f(2, 2)
        nc.sync.dma_start(out=x_raw[0][:], in_=x_view[0])
        load_f(4, 2)
        nc.sync.dma_start(out=x_raw[1][:], in_=x_view[1])
        load_f(6, 2)
        nc.sync.dma_start(out=bias_rows[0 : HID // P, :], in_=b1.rearrange("(j p) -> j p", p=P))
        nc.sync.dma_start(out=w_raw[:], in_=w_view)
        nc.sync.dma_start(out=bias[:], in_=b1.partition_broadcast(P))

        identity_bf = keep.tile([P, P], BF16, name="identity_bf")

        x_width = PACK * FEATS
        x0_and_blocks = keep.tile([P, x_width + PAIR * NODES], BF16, name="x0_and_blocks", align_bytes=64)
        first_codes = keep.tile([P, FEATS + PAIR * PASSES * P], U32, name="first_codes", align_bytes=64)
        first_scales = keep.tile([P, FEATS + PAIR * PASSES * P], U8, name="first_scales", align_bytes=64)
        x_grouped = [x0_and_blocks[:, :x_width], keep.tile([P, x_width], BF16, name="x1_grouped", align_bytes=64)[:]]
        w_grouped = [keep.tile([P, PACK * HALF], BF16, name="w_grouped%d" % half, align_bytes=64)[:] for half in range(2)]
        x_codes = [first_codes[:, :FEATS], keep.tile([P, FEATS], U32, name="x1_codes", align_bytes=64)[:]]
        x_scales = [first_scales[:, :FEATS], keep.tile([P, FEATS], U8, name="x1_scales", align_bytes=64)[:]]
        w_codes = keep.tile([P, HID], U32, name="w_codes", align_bytes=64)
        w_scales = keep.tile([P, HID], U8, name="w_scales", align_bytes=64)
        scaled_pair = [x0_and_blocks[:, x_width:], keep.tile([P, PAIR * NODES], BF16, name="scaled_pair", align_bytes=64)[:]]

        plain = {}
        wide, turned, scaled, f_mx, agg, agg_mx, second, back, biased, result = ({} for unused in range(10))

        def widen(b):
            wide[b] = each.tile([P, NODES], BF16, name="wide", align_bytes=64)
            nc.scalar.copy(out=wide[b][:], in_=raw[b].bitcast(FP8))

        def turn_pass(dst, b, g):
            words = wide[b][:].bitcast(F32)
            for u in range(2):
                nc.tensor.transpose(dst(u), words[:, 2 * P * g + u : 2 * P * (g + 1) : 2], identity[:])

        def turn(b):
            turned[b] = bank(b)
            view = turned[b][:].rearrange("p (u g r) -> p u g r", u=2, g=PASSES)
            for g in range(PASSES):
                turn_pass(lambda u: view[:, u, g, :], b, g)

        def scaled_tile(b):
            if b < 2 * len(scaled_pair):
                return scaled_pair[b // 2][:, (b % 2) * NODES : (b % 2 + 1) * NODES]
            return each.tile([P, NODES], BF16, name="scaled", align_bytes=64)[:]

        def scale_out(b):
            scaled[b] = scaled_tile(b)
            nc.vector.tensor_tensor(
                out=scaled[b].rearrange("p (g r u e) -> p g r u e", g=PASSES, u=2, e=2),
                in0=turned[b][:].bitcast(BF16).rearrange("p (u g r e) -> p g r u e", u=2, g=PASSES, e=2),
                in1=scale[:].rearrange("p g (u e) -> p g u e", e=2).unsqueeze(2).to_broadcast([P, PASSES, P, 2, 2]),
                op=ALU.mult,
            )

        def first_block():
            wide[0] = each.tile([P, NODES], BF16, name="wide", align_bytes=64)
            nc.vector.tensor_copy(out=wide[0][:, :FIRST_ON_VECTOR], in_=first_raw[0][:, :FIRST_ON_VECTOR].bitcast(FP8))
            nc.scalar.copy(out=wide[0][:, FIRST_ON_VECTOR:K_PASS], in_=first_raw[0][:, FIRST_ON_VECTOR:].bitcast(FP8))
            nc.vector.tensor_copy(out=wide[0][:, K_PASS:], in_=first_raw[1][:].bitcast(FP8))
            nc.vector.tensor_copy(out=identity_bf[:], in_=identity[:])
            scaled[0] = scaled_tile(0)
            for g, number in enumerate((0, LAST)):
                pass_bank = bank(number)
                turn_pass(lambda u: pass_bank[:, u * P : (u + 1) * P], 0, g)
                nc.vector.tensor_tensor(
                    out=scaled[0].rearrange("p (g r u e) -> p g r u e", g=PASSES, u=2, e=2)[:, g],
                    in0=pass_bank[:, : 2 * P].bitcast(BF16).rearrange("p (u r e) -> p r u e", u=2, e=2),
                    in1=scale[:, g].rearrange("p (u e) -> p u e", e=2).unsqueeze(1).to_broadcast([P, P, 2, 2]),
                    op=ALU.mult,
                )

        def copy_turned(b):
            plain[b] = keep.tile([P, PASSES, P, PACK], BF16, name="plain%d" % b, align_bytes=64)
            nc.scalar.copy(
                out=plain[b][:].rearrange("p g r t -> p (g r t)").bitcast(F32).rearrange("p (m u) -> p m u", u=2),
                in_=turned[b][:].rearrange("p (u m) -> p m u", u=2),
            )

        def scale_on_gpsimd(b, place):
            scaled[b] = place
            nc.gpsimd.tensor_tensor(
                out=place.rearrange("p (g r t) -> p g r t", g=PASSES, t=PACK),
                in0=plain[b][:],
                in1=scale[:].unsqueeze(2).to_broadcast([P, PASSES, P, PACK]),
                op=ALU.mult,
            )

        def quantize_f(first, count=1):
            width = PASSES * P
            codes = keep.tile([P, count * width], U32, name="f_codes%d" % first, align_bytes=64)
            scales = keep.tile([P, count * width], U8, name="f_scales%d" % first, align_bytes=64)
            source = scaled[first] if count == 1 else scaled_pair[first // 2]
            nc.vector.quantize_mx(out=codes[:].bitcast(FP8X4), scales=scales[:], in_=source)
            for j in range(count):
                f_mx[first + j] = (codes[:, j * width : (j + 1) * width], scales[:, j * width : (j + 1) * width])

        def x_place(g, cols):
            return x_grouped[g].rearrange("p (s m t) -> p m s t", s=PACK, t=PACK)[:, cols.start // PACK : cols.stop // PACK]

        def group_x(copy, g, cols):
            copy(x_place(g, cols), x_raw[g][:, :, cols].rearrange("p t (m s) -> p m s t", s=PACK))

        def group_on_tensor(rows, first, number):
            held = bank(number, BF16, 2 * BANK)
            columns = rows[:].rearrange("p t c -> p c t")
            for q in range(2):
                nc.tensor.matmul(out=held[:, q * BANK : (q + 1) * BANK], lhsT=identity_bf[:], rhs=columns[:, first + q * P : first + (q + 1) * P], start=True, stop=True)
            return held

        def empty_x(g, cols, held):
            nc.scalar.copy(out=x_place(g, cols).rearrange("p m s t -> p s m t"), in_=held[:].rearrange("p (m s t) -> p s m t", s=PACK, t=PACK))

        def quantize_x0_and_blocks():
            nc.vector.quantize_mx(out=first_codes[:].bitcast(FP8X4), scales=first_scales[:], in_=x0_and_blocks[:])
            for b in range(PAIR):
                cols = slice(FEATS + b * PASSES * P, FEATS + (b + 1) * PASSES * P)
                f_mx[b] = (first_codes[:, cols], first_scales[:, cols])

        def quantize_x1():
            nc.vector.quantize_mx(out=x_codes[1].bitcast(FP8X4), scales=x_scales[1], in_=x_grouped[1])

        def group_w(copy, half):
            cols = slice(HALF * half, HALF * (half + 1))
            copy(w_grouped[half].rearrange("p (h t) -> p h t", t=PACK), w_raw[:].rearrange("p t h -> p h t")[:, cols])

        def empty_w(half, held):
            nc.scalar.copy(out=w_grouped[half], in_=held[:])

        def quantize_w(half):
            cols = slice(HALF * half, HALF * (half + 1))
            nc.vector.quantize_mx(out=w_codes[:, cols].bitcast(FP8X4), scales=w_scales[:, cols], in_=w_grouped[half])

        def first_product(b):
            codes, scales = f_mx[b]
            agg[b] = bank(b)
            for s in range(PACK):
                cols = slice(s * P, (s + 1) * P)
                for g in range(PASSES):
                    nodes = slice(g * P, (g + 1) * P)
                    nc.tensor.matmul_mx(
                        out=agg[b][:, cols],
                        lhsT=x_codes[g][:, cols].bitcast(FP8X4),
                        lhsT_scale=x_scales[g][:, cols],
                        rhs=codes[:, nodes].bitcast(FP8X4),
                        rhs_scale=scales[:, nodes],
                        start=(g == 0),
                        stop=(g == PASSES - 1),
                    )

        agg_all = keep.tile([P, BLOCKS, P, PACK], BF16, name="agg_all", align_bytes=64)

        def copy_agg(b):
            nc.scalar.copy(out=agg_all[:, b], in_=agg[b][:].rearrange("p (s r) -> p r s", s=PACK))

        def quantize_agg(first, count=1):
            codes = keep.tile([P, count * P], U32, name="agg_codes%d" % first, align_bytes=64)
            scales = keep.tile([P, count * P], U8, name="agg_scales%d" % first, align_bytes=64)
            source = agg_all[:, first : first + count].rearrange("p b r s -> p (b r s)")
            nc.vector.quantize_mx(out=codes[:].bitcast(FP8X4), scales=scales[:], in_=source)
            for j in range(count):
                agg_mx[first + j] = (codes[:, j * P : (j + 1) * P], scales[:, j * P : (j + 1) * P])
            return codes, scales

        def second_product(b, cols=slice(0, HID), number=None):
            codes, scales = agg_mx[b]
            second[b, cols.start] = bank(b if number is None else number)[:, cols]
            nc.tensor.matmul_mx(
                out=second[b, cols.start],
                lhsT=codes.bitcast(FP8X4),
                lhsT_scale=scales,
                rhs=w_codes[:, cols].bitcast(FP8X4),
                rhs_scale=w_scales[:, cols],
                start=True,
                stop=True,
            )

        def add_bias(b, cols=slice(0, HID)):
            if b not in biased:
                biased[b] = each.tile([P, HID], F32, name="biased")
            nc.vector.tensor_tensor(out=biased[b][:, cols], in0=second[b, cols.start], in1=bias[:, cols], op=ALU.add)

        def finish(b, cols=slice(0, HID)):
            if b not in result:
                result[b] = each.tile([P, HID], F32, name="result")
            nc.scalar.activation(out=result[b][:, cols], in_=biased[b][:, cols], func=ACT.Tanh)
            nc.sync.dma_start(out=out_view[:, b, cols], in_=result[b][:, cols])

        pair_tanh = [keep.tile([P, PAIR * P], F32, name="pair_tanh%d" % j, align_bytes=64) for j in range(HID // P)]

        def pair_product(pair_codes, pair_scales, bias_columns):
            banks = [bank(number) for number in range(PAIR)]
            tiles = [banks[j // 2][:, (j % 2) * PAIR * P : (j % 2 + 1) * PAIR * P] for j in range(HID // P)]
            for j, tile in enumerate(tiles):
                cols = slice(j * P, (j + 1) * P)
                nc.tensor.matmul_mx(
                    out=tile,
                    lhsT=w_codes[:, cols].bitcast(FP8X4),
                    lhsT_scale=w_scales[:, cols],
                    rhs=pair_codes[:].bitcast(FP8X4),
                    rhs_scale=pair_scales[:],
                    start=True,
                    stop=True,
                )
            for j, tile in enumerate(tiles):
                nc.scalar.activation(out=pair_tanh[j][:], in_=tile, func=ACT.Tanh, bias=bias_columns[:, j : j + 1])

        def turn_back(b):
            back[b] = bank(b)
            for j in range(HID // P):
                nc.tensor.transpose(back[b][:, j * P : (j + 1) * P], pair_tanh[j][:, b * P : (b + 1) * P], identity[:])

        def store_turned(b, copy):
            result[b] = each.tile([P, HID], F32, name="result")
            copy(out=result[b][:], in_=back[b][:])
            nc.sync.dma_start(out=out_view[:, b, :], in_=result[b][:])

        def scalar_copy(dst, src):
            nc.scalar.copy(out=dst, in_=src)

        def warm_up(width, target):
            nc.tensor.matmul(out=target[:, :width], lhsT=zeros[:, :P], rhs=zeros[:, :width], start=True, stop=True)

        warm = bank(6)
        for unused in range(2):
            warm_up(WARM_FIRST, warm)
        first_block()
        warm_up(WARM_TINY, warm)
        for blocks in ((1,), (2, 3)):
            for b in blocks:
                widen(b)
                turn(b)
                scale_out(b)
            warm_up(WARM_SHORT if blocks == (1,) else WARM_BETWEEN, warm)
        halves = [slice(HALF * half, HALF * (half + 1)) for half in range(2)]
        group_x(gpsimd_copy, 0, slice(0, X_COLUMNS_ON_GPSIMD))
        group_x(scalar_copy, 0, slice(X_COLUMNS_ON_GPSIMD, FEATS))
        for b in (4, 5):
            widen(b)
        group_x(scalar_copy, 1, halves[1])
        empty_x(1, halves[0], group_on_tensor(x_raw[1], 0, 0))
        for b in (4, 5):
            turn(b)
        bias_turned = bank(2, BF16, 2 * BANK)
        nc.tensor.transpose(bias_turned[:, :P], bias_rows[:], identity_bf[:])
        w_held = group_on_tensor(w_raw, 0, LAST)
        widen(6)
        turn(6)
        copy_turned(5)
        widen(LAST)
        empty_w(0, w_held)
        bias_columns = keep.tile([P, HID // P], F32, name="bias_columns")
        nc.scalar.copy(out=bias_columns[:], in_=bias_turned[:, : HID // P])
        group_w(scalar_copy, 1)
        quantize_x0_and_blocks()
        quantize_x1()
        quantize_f(2, PAIR)
        scale_on_gpsimd(5, x_grouped[1][:, :NODES])
        for b in (4, 6):
            scale_out(b)
        quantize_f(4)
        for b in range(5):
            if b == 4:
                turn(LAST)
            first_product(b)
            copy_agg(b)
        quantize_w(0)
        pair_codes, pair_scales = quantize_agg(0, PAIR)
        quantize_w(1)
        pair_product(pair_codes, pair_scales, bias_columns)
        quantize_f(5)
        quantize_f(6)
        quantize_agg(2, 2)
        first_product(5)
        second_product(2)
        first_product(6)
        second_product(3)
        scale_out(LAST)
        add_bias(2)
        quantize_f(LAST)
        quantize_agg(4)
        add_bias(3)
        copy_agg(5)
        finish(2)
        copy_agg(6)
        for b in range(PAIR):
            turn_back(b)
        first_product(LAST)
        second_product(4)
        quantize_agg(5)
        second_product(5)
        store_turned(0, nc.vector.tensor_copy)
        quantize_agg(6)
        second_product(6)
        store_turned(1, nc.scalar.copy)
        copy_agg(LAST)
        warm_up(WARM_LAST, bank(2))
        finish(3)
        for b in (4, 5):
            add_bias(b)
            finish(b)
        quantize_agg(LAST)
        for cols, number in zip(halves, (LAST, 0)):
            second_product(LAST, cols, number)
        add_bias(6)
        finish(6)
        for cols in halves:
            add_bias(LAST, cols)
            finish(LAST, cols)
